import numpy as np
import ml_dtypes


def mxq(x, axis, fmt="e4m3"):
    dtype, down = {"e4m3": (ml_dtypes.float8_e4m3fn, 7), "e5m2": (ml_dtypes.float8_e5m2, 14)}[fmt]
    v = np.moveaxis(np.asarray(x, np.float32).astype(ml_dtypes.bfloat16).astype(np.float64), axis, -1)
    blocks = v.reshape(v.shape[:-1] + (-1, 32))
    amax = np.abs(blocks).max(-1, keepdims=True)
    byte = np.maximum(np.where(amax > 0, np.frexp(amax)[1] - 1 + 127, 0) - down, 1)
    scale = np.exp2(byte - 127.0)
    codes = (blocks / scale).astype(np.float32).astype(dtype).astype(np.float64)
    return np.moveaxis((codes * scale).reshape(v.shape), -1, axis)


WIDE = False


def mx_kscale(k):
    if not WIDE:
        return np.ones(k)
    levels = np.array([10, -10, 5, -5, 0])
    a = np.random.permutation(np.resize(levels, k // 512 * 4)).reshape(k // 512, 4)
    idx = np.arange(k)
    return np.exp2(a[idx // 512, idx % 128 // 32])


BF16 = ml_dtypes.bfloat16


def bf(x):
    return np.asarray(x, np.float32).astype(BF16)


def f64(x):
    return np.asarray(x).astype(np.float64)


N, IN, HID, OUT, MLP, NF = 128, 256, 512, 512, 512, 8
FS = N // NF


def draw_hiddens():
    amp = 0.2 + 0.8 * np.random.random((N, 1))
    centre = np.repeat(np.random.standard_normal((NF, HID)), FS, axis=0)
    return amp * np.random.standard_normal((N, HID)) + 0.3 * centre


def setup_inputs():
    s, t = mx_kscale(HID), mx_kscale(MLP)
    c1 = 1.2 / np.sqrt(IN + HID)
    cx = 1.2 * np.sqrt(IN / (IN + HID))
    c2 = 2.0 / np.sqrt(MLP)
    return {
        "hiddens": bf(draw_hiddens() * s),
        "Wa1h": bf(np.random.standard_normal((MLP, HID)) * c1 * t[:, None] / s),
        "drive_a": bf(np.random.standard_normal(MLP) * cx * t),
        "Wa2": bf(np.random.standard_normal((OUT, MLP)) * c2 / t),
        "ba2": bf(np.random.standard_normal(OUT) * 0.1),
        "Wg1h": bf(np.random.standard_normal((MLP, HID)) * c1 * t[:, None] / s),
        "drive_g": bf(np.random.standard_normal(MLP) * cx * t),
        "Wg2": bf(np.random.standard_normal((OUT, MLP)) * c2 / t),
        "bg2": bf(np.random.standard_normal(OUT) * 0.1),
    }


def engine(hq, w1h, drive, w2, b2):
    u = np.maximum((hq @ mxq(f64(w1h), 1, "e4m3").T) + f64(drive), 0.0)
    return (mxq(u, 1, "e4m3") @ mxq(f64(w2), 1, "e4m3").T) + f64(b2)


def reference(hiddens, Wa1h, drive_a, Wa2, ba2, Wg1h, drive_g, Wg2, bg2):
    hq = mxq(f64(hiddens), 1, "e4m3")
    a = engine(hq, Wa1h, drive_a, Wa2, ba2)
    g = engine(hq, Wg1h, drive_g, Wg2, bg2)
    diff = a - g
    tension = np.mean(diff * diff, axis=-1, keepdims=True)
    t0 = tension[:, 0]
    e = np.exp(t0 - t0.max())
    w = e / e.sum()
    combined = (w[:, None] * diff).sum(axis=0, keepdims=True)
    mean_tension = tension.mean(axis=0)
    return diff, tension, combined, mean_tension

@@ -1,0 +1,240 @@
+from contextlib import ExitStack
+import math
+
+import concourse.mybir as mybir
+from concourse.masks import make_identity
+
+F32 = mybir.dt.float32
+BF16 = mybir.dt.bfloat16
+U32 = mybir.dt.uint32
+U8 = mybir.dt.uint8
+FP8X4 = mybir.dt.float8_e4m3fn_x4
+ACT = mybir.ActivationFunctionType
+ALU = mybir.AluOpType
+AXIS = mybir.AxisListType
+
+P = 128
+PACK = 4
+K = P * PACK
+OUT = 512
+BLOCKS = 4
+HALVES = 2
+BANK = 512
+PAIR = 2 * P
+
+FLOPS = 4 * 2 * P * K * 512 + 2 * P * OUT
+
+
+def transpose_words(nc, bank, first, rows_bf16, ident):
+    words = rows_bf16.bitcast(F32)
+    for half in range(HALVES):
+        nc.tensor.transpose(
+            bank[:, first + half * P : first + (half + 1) * P],
+            words[:, half * P : (half + 1) * P],
+            ident[:],
+        )
+
+
+def pack_weight(nc, pools, ident, label, w_sb, codes, scales):
+    grouped = pools["sbuf"].tile([P, BLOCKS * P * PACK], BF16, align_bytes=64, name="grouped_%s" % label)
+    for pair in range(BLOCKS // 2):
+        bank = pools["bank"].tile([P, BANK], F32, tag="bank")
+        for b in range(2):
+            block = 2 * pair + b
+            transpose_words(nc, bank, b * PAIR, w_sb[:, block * K : (block + 1) * K], ident)
+        source = bank[:].rearrange("p (b half r) -> p b r half", b=2, half=HALVES)
+        target = (
+            grouped[:, pair * PAIR * PACK : (pair + 1) * PAIR * PACK]
+            .bitcast(F32)
+            .rearrange("p (b r half) -> p b r half", b=2, half=HALVES)
+        )
+        if pair % 2 == 0:
+            nc.scalar.copy(out=target, in_=source)
+        else:
+            nc.vector.tensor_copy(out=target, in_=source)
+    for pair in range(BLOCKS // 2):
+        cols = slice(pair * PAIR, (pair + 1) * PAIR)
+        nc.vector.quantize_mx(
+            out=codes[:, cols].bitcast(FP8X4),
+            scales=scales[:, cols],
+            in_=grouped[:, pair * PAIR * PACK : (pair + 1) * PAIR * PACK],
+        )
+
+
+def first_layer(nc, pools, label, w1_codes, w1_scales, h_codes, h_scales, drive, u_codes, u_scales):
+    z = pools["z"].tile([P, BLOCKS * P], F32, tag="z")
+    for t in range(BLOCKS):
+        cols = slice(t * P, (t + 1) * P)
+        nc.tensor.matmul_mx(
+            out=z[:, cols],
+            lhsT=w1_codes[:, cols].bitcast(FP8X4),
+            lhsT_scale=w1_scales[:, cols],
+            rhs=h_codes[:].bitcast(FP8X4),
+            rhs_scale=h_scales[:],
+            start=True,
+            stop=True,
+        )
+    planes = pools["sbuf"].tile([P, BLOCKS * P], BF16, name="planes_%s" % label)
+    for t in range(BLOCKS):
+        cols = slice(t * P, (t + 1) * P)
+        nc.scalar.activation(out=planes[:, cols], in_=z[:, cols], func=ACT.Relu, bias=drive[:, t : t + 1], scale=1.0)
+    grouped = pools["sbuf"].tile([P, P * PACK], BF16, align_bytes=64, name="grouped_u_%s" % label)
+    nc.vector.tensor_copy(
+        out=grouped[:].rearrange("p (c t) -> p c t", t=PACK),
+        in_=planes[:].rearrange("p (t c) -> p c t", t=PACK),
+    )
+    nc.vector.quantize_mx(out=u_codes[:].bitcast(FP8X4), scales=u_scales[:], in_=grouped[:])
+
+
+def second_layer(nc, pools, u_codes, u_scales, w2_codes, w2_scales):
+    acc = pools["acc"].tile([P, OUT], F32, tag="acc")
+    for pair in range(BLOCKS // 2):
+        cols = slice(pair * PAIR, (pair + 1) * PAIR)
+        nc.tensor.matmul_mx(
+            out=acc[:, cols],
+            lhsT=u_codes[:].bitcast(FP8X4),
+            lhsT_scale=u_scales[:],
+            rhs=w2_codes[:, cols].bitcast(FP8X4),
+            rhs_scale=w2_scales[:, cols],
+            start=True,
+            stop=True,
+        )
+    return acc
+
+
+def tile_phiaslossengine_pa_s_kernel(
+    tc, hiddens, Wa1h, drive_a, Wa2, ba2, Wg1h, drive_g, Wg2, bg2, out_0, out_1, out_2, out_3
+):
+    nc = tc.nc
+    with ExitStack() as ctx:
+        pools = {
+            "sbuf": ctx.enter_context(tc.tile_pool(name="sbuf", bufs=1)),
+            "bank": ctx.enter_context(tc.psum_pool(name="bank", bufs=4)),
+            "z": ctx.enter_context(tc.psum_pool(name="z", bufs=2)),
+            "acc": ctx.enter_context(tc.psum_pool(name="acc", bufs=2)),
+        }
+        sbuf = pools["sbuf"]
+
+        h_sb = sbuf.tile([P, K], BF16)
+        nc.sync.dma_start(out=h_sb[:], in_=hiddens)
+        w_sb = {}
+        for label, w in (("a1", Wa1h), ("g1", Wg1h)):
+            w_sb[label] = sbuf.tile([P, BLOCKS * K], BF16, name="w_%s" % label)
+            nc.sync.dma_start(
+                out=w_sb[label][:].rearrange("p (half ek) -> p half ek", half=HALVES),
+                in_=w.rearrange("(half p e) k -> p half (e k)", half=HALVES, e=2),
+            )
+        for label, w in (("a2", Wa2), ("g2", Wg2)):
+            w_sb[label] = sbuf.tile([P, BLOCKS * K], BF16, name="w_%s" % label)
+            nc.sync.dma_start(out=w_sb[label][:], in_=w.rearrange("(c r) k -> c (r k)", r=BLOCKS))
+
+        small_bf16 = {}
+        with nc.allow_non_contiguous_dma(reason="512 values spread over 128 partitions"):
+            for label, v in (("da", drive_a), ("dg", drive_g)):
+                small_bf16[label] = sbuf.tile([P, BLOCKS], BF16, name="small_%s" % label)
+                nc.scalar.dma_start(
+                    out=small_bf16[label][:].rearrange("p (half e) -> p half e", half=HALVES),
+                    in_=v.rearrange("(half p e) -> p half e", half=HALVES, e=2),
+                )
+            for label, v in (("ba", ba2), ("bg", bg2)):
+                small_bf16[label] = sbuf.tile([P, BLOCKS], BF16, name="small_%s" % label)
+                nc.scalar.dma_start(out=small_bf16[label][:], in_=v.rearrange("(c r) -> c r", r=BLOCKS))
+
+        ident = sbuf.tile([P, P], F32)
+        make_identity(nc, ident[:])
+        warm = sbuf.tile([P, 1], F32)
+        nc.vector.memset(warm[:], 0.0)
+        nc.scalar.activation(out=warm[:], in_=warm[:], func=ACT.Exp)
+
+        drive_f32 = {}
+        for label in ("da", "dg"):
+            drive_f32[label] = sbuf.tile([P, BLOCKS], F32, name="drive_%s" % label)
+            nc.gpsimd.tensor_copy(out=drive_f32[label][:], in_=small_bf16[label][:])
+        bias_col = sbuf.tile([P, BLOCKS], F32)
+        nc.gpsimd.tensor_tensor(out=bias_col[:], in0=small_bf16["ba"][:], in1=small_bf16["bg"][:], op=ALU.subtract)
+
+        codes = {}
+        scales = {}
+        for label in ("a1", "g1", "a2", "g2"):
+            codes[label] = sbuf.tile([P, BLOCKS * P], U32, align_bytes=64, name="codes_%s" % label)
+            scales[label] = sbuf.tile([P, BLOCKS * P], U8, align_bytes=64, name="scales_%s" % label)
+        for label in ("h", "ua", "ug"):
+            codes[label] = sbuf.tile([P, P], U32, align_bytes=64, name="codes_%s" % label)
+            scales[label] = sbuf.tile([P, P], U8, align_bytes=64, name="scales_%s" % label)
+
+        h_bank = pools["bank"].tile([P, BANK], F32, tag="bank")
+        transpose_words(nc, h_bank, 0, h_sb[:], ident)
+        h_grouped = sbuf.tile([P, P * PACK], BF16, align_bytes=64)
+        nc.vector.tensor_copy(
+            out=h_grouped[:].bitcast(F32).rearrange("p (c half) -> p c half", half=HALVES),
+            in_=h_bank[:, 0:PAIR].rearrange("p (half c) -> p c half", half=HALVES),
+        )
+        nc.vector.quantize_mx(out=codes["h"][:].bitcast(FP8X4), scales=scales["h"][:], in_=h_grouped[:])
+
+        pack_weight(nc, pools, ident, "a1", w_sb["a1"], codes["a1"], scales["a1"])
+        first_layer(nc, pools, "a", codes["a1"], scales["a1"], codes["h"], scales["h"], drive_f32["da"], codes["ua"], scales["ua"])
+        pack_weight(nc, pools, ident, "g1", w_sb["g1"], codes["g1"], scales["g1"])
+        first_layer(nc, pools, "g", codes["g1"], scales["g1"], codes["h"], scales["h"], drive_f32["dg"], codes["ug"], scales["ug"])
+
+        bias_bank = pools["bank"].tile([P, BANK], F32, tag="bank")
+        for r in range(BLOCKS):
+            nc.tensor.transpose(bias_bank[:, r * P : (r + 1) * P], bias_col[:, r : r + 1].to_broadcast([P, P]), ident[:])
+        bias_rows = sbuf.tile([P, OUT], F32)
+        nc.scalar.copy(
+            out=bias_rows[:].rearrange("p (c r) -> p c r", r=BLOCKS),
+            in_=bias_bank[:].rearrange("p (r c) -> p c r", r=BLOCKS),
+        )
+
+        pack_weight(nc, pools, ident, "a2", w_sb["a2"], codes["a2"], scales["a2"])
+        acc_a = second_layer(nc, pools, codes["ua"], scales["ua"], codes["a2"], scales["a2"])
+        a_sb = sbuf.tile([P, OUT], F32)
+        nc.vector.tensor_tensor(
+            out=a_sb[:].rearrange("p (c r) -> p c r", r=BLOCKS),
+            in0=acc_a[:].rearrange("p (r c) -> p c r", r=BLOCKS),
+            in1=bias_rows[:].rearrange("p (c r) -> p c r", r=BLOCKS),
+            op=ALU.add,
+        )
+        pack_weight(nc, pools, ident, "g2", w_sb["g2"], codes["g2"], scales["g2"])
+        acc_g = second_layer(nc, pools, codes["ug"], scales["ug"], codes["g2"], scales["g2"])
+        diff = sbuf.tile([P, OUT], F32)
+        nc.vector.tensor_tensor(
+            out=diff[:].rearrange("p (c r) -> p c r", r=BLOCKS),
+            in0=a_sb[:].rearrange("p (c r) -> p c r", r=BLOCKS),
+            in1=acc_g[:].rearrange("p (r c) -> p c r", r=BLOCKS),
+            op=ALU.subtract,
+        )
+        nc.sync.dma_start(out=out_0, in_=diff[:])
+
+        squares = sbuf.tile([P, OUT], F32)
+        tension = sbuf.tile([P, 1], F32)
+        nc.scalar.activation(
+            out=squares[:], in_=diff[:], func=ACT.Square, scale=1.0 / math.sqrt(OUT), accum_out=tension[:]
+        )
+        t_bank = pools["bank"].tile([P, BANK], F32, tag="bank")
+        nc.tensor.transpose(t_bank[:, 0:P], tension[:, 0:1].to_broadcast([P, P]), ident[:])
+        neg_max = sbuf.tile([P, 1], F32)
+        nc.vector.tensor_reduce(out=neg_max[:], in_=t_bank[:, 0:P], axis=AXIS.X, op=ALU.max, negate=True)
+
+        e_col = sbuf.tile([P, 1], F32)
+        nc.scalar.activation(out=e_col[:], in_=tension[:], func=ACT.Exp, bias=neg_max[:], scale=1.0)
+        comb_bank = pools["bank"].tile([P, BANK], F32, tag="bank")
+        nc.tensor.matmul(out=comb_bank[:], lhsT=e_col[:, 0:1].to_broadcast([P, P]), rhs=diff[:], start=True, stop=True)
+
+        t_rows = sbuf.tile([P, P], F32)
+        nc.vector.tensor_copy(out=t_rows[:], in_=t_bank[:, 0:P])
+        nc.sync.dma_start(out=out_1.rearrange("n o -> o n"), in_=t_rows[0:1, :])
+        e_rows = sbuf.tile([P, P], F32)
+        e_sum = sbuf.tile([P, 1], F32)
+        nc.scalar.activation(out=e_rows[:], in_=t_rows[:], func=ACT.Exp, bias=neg_max[:], scale=1.0, accum_out=e_sum[:])
+        inv_sum = sbuf.tile([P, 1], F32)
+        nc.vector.reciprocal(out=inv_sum[:], in_=e_sum[:])
+
+        t_sum = sbuf.tile([P, 1], F32)
+        nc.vector.tensor_reduce(out=t_sum[:], in_=t_rows[:], axis=AXIS.X, op=ALU.add)
+        t_mean = sbuf.tile([P, 1], F32)
+        nc.vector.tensor_scalar_mul(out=t_mean[:], in0=t_sum[:], scalar1=1.0 / P)
+        nc.sync.dma_start(out=out_3.rearrange("(o n) -> o n", o=1), in_=t_mean[0:1, :])
+
+        combined = sbuf.tile([P, OUT], F32)
+        nc.vector.tensor_scalar_mul(out=combined[:], in0=comb_bank[:], scalar1=inv_sum[:, 0:1])
+        nc.sync.dma_start(out=out_2, in_=combined[0:1, :])

@@ -17,192 +17,190 @@ P = 128
 PACK = 4
 K = P * PACK
 OUT = 512
-BLOCKS = 4
 HALVES = 2
-BANK = 512
 PAIR = 2 * P
+BANK = 512
 
 FLOPS = 4 * 2 * P * K * 512 + 2 * P * OUT
-
-
-def transpose_words(nc, bank, first, rows_bf16, ident):
-    words = rows_bf16.bitcast(F32)
-    for half in range(HALVES):
-        nc.tensor.transpose(
-            bank[:, first + half * P : first + (half + 1) * P],
-            words[:, half * P : (half + 1) * P],
-            ident[:],
-        )
-
-
-def pack_weight(nc, pools, ident, label, w_sb, codes, scales):
-    grouped = pools["sbuf"].tile([P, BLOCKS * P * PACK], BF16, align_bytes=64, name="grouped_%s" % label)
-    for pair in range(BLOCKS // 2):
-        bank = pools["bank"].tile([P, BANK], F32, tag="bank")
-        for b in range(2):
-            block = 2 * pair + b
-            transpose_words(nc, bank, b * PAIR, w_sb[:, block * K : (block + 1) * K], ident)
-        source = bank[:].rearrange("p (b half r) -> p b r half", b=2, half=HALVES)
-        target = (
-            grouped[:, pair * PAIR * PACK : (pair + 1) * PAIR * PACK]
-            .bitcast(F32)
-            .rearrange("p (b r half) -> p b r half", b=2, half=HALVES)
-        )
-        if pair % 2 == 0:
-            nc.scalar.copy(out=target, in_=source)
-        else:
-            nc.vector.tensor_copy(out=target, in_=source)
-    for pair in range(BLOCKS // 2):
-        cols = slice(pair * PAIR, (pair + 1) * PAIR)
-        nc.vector.quantize_mx(
-            out=codes[:, cols].bitcast(FP8X4),
-            scales=scales[:, cols],
-            in_=grouped[:, pair * PAIR * PACK : (pair + 1) * PAIR * PACK],
-        )
-
-
-def first_layer(nc, pools, label, w1_codes, w1_scales, h_codes, h_scales, drive, u_codes, u_scales):
-    z = pools["z"].tile([P, BLOCKS * P], F32, tag="z")
-    for t in range(BLOCKS):
-        cols = slice(t * P, (t + 1) * P)
-        nc.tensor.matmul_mx(
-            out=z[:, cols],
-            lhsT=w1_codes[:, cols].bitcast(FP8X4),
-            lhsT_scale=w1_scales[:, cols],
-            rhs=h_codes[:].bitcast(FP8X4),
-            rhs_scale=h_scales[:],
-            start=True,
-            stop=True,
-        )
-    planes = pools["sbuf"].tile([P, BLOCKS * P], BF16, name="planes_%s" % label)
-    for t in range(BLOCKS):
-        cols = slice(t * P, (t + 1) * P)
-        nc.scalar.activation(out=planes[:, cols], in_=z[:, cols], func=ACT.Relu, bias=drive[:, t : t + 1], scale=1.0)
-    grouped = pools["sbuf"].tile([P, P * PACK], BF16, align_bytes=64, name="grouped_u_%s" % label)
-    nc.vector.tensor_copy(
-        out=grouped[:].rearrange("p (c t) -> p c t", t=PACK),
-        in_=planes[:].rearrange("p (t c) -> p c t", t=PACK),
-    )
-    nc.vector.quantize_mx(out=u_codes[:].bitcast(FP8X4), scales=u_scales[:], in_=grouped[:])
-
-
-def second_layer(nc, pools, u_codes, u_scales, w2_codes, w2_scales):
-    acc = pools["acc"].tile([P, OUT], F32, tag="acc")
-    for pair in range(BLOCKS // 2):
-        cols = slice(pair * PAIR, (pair + 1) * PAIR)
-        nc.tensor.matmul_mx(
-            out=acc[:, cols],
-            lhsT=u_codes[:].bitcast(FP8X4),
-            lhsT_scale=u_scales[:],
-            rhs=w2_codes[:, cols].bitcast(FP8X4),
-            rhs_scale=w2_scales[:, cols],
-            start=True,
-            stop=True,
-        )
-    return acc
 
 
 def tile_phiaslossengine_pa_s_kernel(
     tc, hiddens, Wa1h, drive_a, Wa2, ba2, Wg1h, drive_g, Wg2, bg2, out_0, out_1, out_2, out_3
 ):
     nc = tc.nc
+    weights = {"a1": Wa1h, "g1": Wg1h, "a2": Wa2, "g2": Wg2}
     with ExitStack() as ctx:
-        pools = {
-            "sbuf": ctx.enter_context(tc.tile_pool(name="sbuf", bufs=1)),
-            "bank": ctx.enter_context(tc.psum_pool(name="bank", bufs=4)),
-            "z": ctx.enter_context(tc.psum_pool(name="z", bufs=2)),
-            "acc": ctx.enter_context(tc.psum_pool(name="acc", bufs=2)),
-        }
-        sbuf = pools["sbuf"]
+        ctx.enter_context(tc.manual_schedule())
+        sbuf = ctx.enter_context(tc.tile_pool(name="sbuf", bufs=1))
+        banks = ctx.enter_context(tc.psum_pool(name="banks", bufs=4))
+        z_pool = ctx.enter_context(tc.psum_pool(name="z", bufs=2))
+        acc_pool = ctx.enter_context(tc.psum_pool(name="acc", bufs=2))
 
         h_sb = sbuf.tile([P, K], BF16)
         nc.sync.dma_start(out=h_sb[:], in_=hiddens)
         w_sb = {}
-        for label, w in (("a1", Wa1h), ("g1", Wg1h)):
-            w_sb[label] = sbuf.tile([P, BLOCKS * K], BF16, name="w_%s" % label)
-            nc.sync.dma_start(
-                out=w_sb[label][:].rearrange("p (half ek) -> p half ek", half=HALVES),
-                in_=w.rearrange("(half p e) k -> p half (e k)", half=HALVES, e=2),
-            )
-        for label, w in (("a2", Wa2), ("g2", Wg2)):
-            w_sb[label] = sbuf.tile([P, BLOCKS * K], BF16, name="w_%s" % label)
-            nc.sync.dma_start(out=w_sb[label][:], in_=w.rearrange("(c r) k -> c (r k)", r=BLOCKS))
-
-        small_bf16 = {}
-        with nc.allow_non_contiguous_dma(reason="512 values spread over 128 partitions"):
-            for label, v in (("da", drive_a), ("dg", drive_g)):
-                small_bf16[label] = sbuf.tile([P, BLOCKS], BF16, name="small_%s" % label)
-                nc.scalar.dma_start(
-                    out=small_bf16[label][:].rearrange("p (half e) -> p half e", half=HALVES),
-                    in_=v.rearrange("(half p e) -> p half e", half=HALVES, e=2),
+        for label in ("a1", "g1", "a2", "g2"):
+            w_sb[label] = sbuf.tile([P, HALVES * 2 * K], BF16, name="w_%s" % label)
+            for half in range(HALVES):
+                nc.sync.dma_start(
+                    out=w_sb[label][:, half * 2 * K : (half + 1) * 2 * K],
+                    in_=weights[label][half * PAIR : (half + 1) * PAIR, :].rearrange("(p e) k -> p (e k)", e=2),
                 )
-            for label, v in (("ba", ba2), ("bg", bg2)):
-                small_bf16[label] = sbuf.tile([P, BLOCKS], BF16, name="small_%s" % label)
-                nc.scalar.dma_start(out=small_bf16[label][:], in_=v.rearrange("(c r) -> c r", r=BLOCKS))
+        small = {}
+        with nc.allow_non_contiguous_dma(reason="512 values spread over 128 partitions"):
+            for label, vector in (("ba", ba2), ("bg", bg2), ("da", drive_a), ("dg", drive_g)):
+                small[label] = sbuf.tile([P, PACK], BF16, name="small_%s" % label)
+                nc.scalar.dma_start(
+                    out=small[label][:].rearrange("p (half e) -> p half e", half=HALVES),
+                    in_=vector.rearrange("(half p e) -> p half e", half=HALVES, e=2),
+                )
 
         ident = sbuf.tile([P, P], F32)
         make_identity(nc, ident[:])
         warm = sbuf.tile([P, 1], F32)
         nc.vector.memset(warm[:], 0.0)
         nc.scalar.activation(out=warm[:], in_=warm[:], func=ACT.Exp)
+        drive = {}
+        for net, label in (("a", "da"), ("g", "dg")):
+            drive[net] = sbuf.tile([P, PACK], F32, name="drive_%s" % net)
+            nc.gpsimd.tensor_copy(out=drive[net][:], in_=small[label][:])
 
-        drive_f32 = {}
-        for label in ("da", "dg"):
-            drive_f32[label] = sbuf.tile([P, BLOCKS], F32, name="drive_%s" % label)
-            nc.gpsimd.tensor_copy(out=drive_f32[label][:], in_=small_bf16[label][:])
-        bias_col = sbuf.tile([P, BLOCKS], F32)
-        nc.gpsimd.tensor_tensor(out=bias_col[:], in0=small_bf16["ba"][:], in1=small_bf16["bg"][:], op=ALU.subtract)
-
+        grouped = {}
         codes = {}
         scales = {}
-        for label in ("a1", "g1", "a2", "g2"):
-            codes[label] = sbuf.tile([P, BLOCKS * P], U32, align_bytes=64, name="codes_%s" % label)
-            scales[label] = sbuf.tile([P, BLOCKS * P], U8, align_bytes=64, name="scales_%s" % label)
-        for label in ("h", "ua", "ug"):
-            codes[label] = sbuf.tile([P, P], U32, align_bytes=64, name="codes_%s" % label)
-            scales[label] = sbuf.tile([P, P], U8, align_bytes=64, name="scales_%s" % label)
+        for label, columns in (("h", P), ("ua", P), ("ug", P), ("a1", K), ("g1", K), ("a2", OUT), ("g2", OUT)):
+            grouped[label] = sbuf.tile([P, columns * PACK], BF16, align_bytes=64, name="grouped_%s" % label)
+            codes[label] = sbuf.tile([P, columns], U32, align_bytes=64, name="codes_%s" % label)
+            scales[label] = sbuf.tile([P, columns], U8, align_bytes=64, name="scales_%s" % label)
 
-        h_bank = pools["bank"].tile([P, BANK], F32, tag="bank")
-        transpose_words(nc, h_bank, 0, h_sb[:], ident)
-        h_grouped = sbuf.tile([P, P * PACK], BF16, align_bytes=64)
+        def transpose_words(bank, first, rows_bf16):
+            words = rows_bf16.bitcast(F32)
+            for khalf in range(HALVES):
+                nc.tensor.transpose(
+                    bank[:, first + khalf * P : first + (khalf + 1) * P], words[:, khalf * P : (khalf + 1) * P], ident[:]
+                )
+
+        def transpose_half(label, half, engine_copy):
+            bank = banks.tile([P, BANK], F32, tag="bank")
+            for e in range(2):
+                block = 2 * half + e
+                transpose_words(bank, e * PAIR, w_sb[label][:, block * K : (block + 1) * K])
+            engine_copy(
+                out=grouped[label][:, half * PAIR * PACK : (half + 1) * PAIR * PACK]
+                .bitcast(F32)
+                .rearrange("p (e r khalf) -> p e r khalf", e=2, khalf=HALVES),
+                in_=bank[:].rearrange("p (e khalf r) -> p e r khalf", e=2, khalf=HALVES),
+            )
+
+        def quantise(label, first, columns):
+            nc.vector.quantize_mx(
+                out=codes[label][:, first : first + columns].bitcast(FP8X4),
+                scales=scales[label][:, first : first + columns],
+                in_=grouped[label][:, first * PACK : (first + columns) * PACK],
+            )
+
+        def quantise_half(label, half):
+            quantise(label, half * PAIR, PAIR)
+
+        planes = {}
+
+        def first_layer(net):
+            w1 = net + "1"
+            z = z_pool.tile([P, PACK * P], F32, tag="z")
+            for t in range(PACK):
+                cols = slice(t * P, (t + 1) * P)
+                nc.tensor.matmul_mx(
+                    out=z[:, cols],
+                    lhsT=codes[w1][:, cols].bitcast(FP8X4),
+                    lhsT_scale=scales[w1][:, cols],
+                    rhs=codes["h"][:].bitcast(FP8X4),
+                    rhs_scale=scales["h"][:],
+                    start=True,
+                    stop=True,
+                )
+            planes[net] = sbuf.tile([P, PACK * P], BF16, name="planes_%s" % net)
+            for t in range(PACK):
+                cols = slice(t * P, (t + 1) * P)
+                nc.scalar.activation(
+                    out=planes[net][:, cols], in_=z[:, cols], func=ACT.Relu, bias=drive[net][:, t : t + 1], scale=1.0
+                )
+
+        def group_hidden(net, sign):
+            nc.vector.tensor_scalar_mul(
+                out=grouped["u" + net][:].rearrange("p (c t) -> p c t", t=PACK),
+                in0=planes[net][:].rearrange("p (t c) -> p c t", t=PACK),
+                scalar1=sign,
+            )
+
+        acc = {}
+
+        def second_layer(net, half, start, stop):
+            cols = slice(half * PAIR, (half + 1) * PAIR)
+            nc.tensor.matmul_mx(
+                out=acc[half][:],
+                lhsT=codes["u" + net][:].bitcast(FP8X4),
+                lhsT_scale=scales["u" + net][:],
+                rhs=codes[net + "2"][:, cols].bitcast(FP8X4),
+                rhs_scale=scales[net + "2"][:, cols],
+                start=start,
+                stop=stop,
+            )
+
+        h_bank = banks.tile([P, BANK], F32, tag="bank")
+        transpose_words(h_bank, 0, h_sb[:])
         nc.vector.tensor_copy(
-            out=h_grouped[:].bitcast(F32).rearrange("p (c half) -> p c half", half=HALVES),
-            in_=h_bank[:, 0:PAIR].rearrange("p (half c) -> p c half", half=HALVES),
+            out=grouped["h"][:].bitcast(F32).rearrange("p (c khalf) -> p c khalf", khalf=HALVES),
+            in_=h_bank[:, 0:PAIR].rearrange("p (khalf c) -> p c khalf", khalf=HALVES),
         )
-        nc.vector.quantize_mx(out=codes["h"][:].bitcast(FP8X4), scales=scales["h"][:], in_=h_grouped[:])
+        transpose_half("a1", 0, nc.scalar.copy)
 
-        pack_weight(nc, pools, ident, "a1", w_sb["a1"], codes["a1"], scales["a1"])
-        first_layer(nc, pools, "a", codes["a1"], scales["a1"], codes["h"], scales["h"], drive_f32["da"], codes["ua"], scales["ua"])
-        pack_weight(nc, pools, ident, "g1", w_sb["g1"], codes["g1"], scales["g1"])
-        first_layer(nc, pools, "g", codes["g1"], scales["g1"], codes["h"], scales["h"], drive_f32["dg"], codes["ug"], scales["ug"])
-
-        bias_bank = pools["bank"].tile([P, BANK], F32, tag="bank")
-        for r in range(BLOCKS):
-            nc.tensor.transpose(bias_bank[:, r * P : (r + 1) * P], bias_col[:, r : r + 1].to_broadcast([P, P]), ident[:])
+        bias_col = sbuf.tile([P, PACK], F32)
+        nc.vector.tensor_tensor(out=bias_col[:], in0=small["ba"][:], in1=small["bg"][:], op=ALU.subtract)
+        bias_bank = banks.tile([P, BANK], F32, tag="bank")
+        for t in range(PACK):
+            nc.tensor.transpose(bias_bank[:, t * P : (t + 1) * P], bias_col[:, t : t + 1].to_broadcast([P, P]), ident[:])
+        quantise("h", 0, P)
         bias_rows = sbuf.tile([P, OUT], F32)
-        nc.scalar.copy(
-            out=bias_rows[:].rearrange("p (c r) -> p c r", r=BLOCKS),
-            in_=bias_bank[:].rearrange("p (r c) -> p c r", r=BLOCKS),
+        nc.vector.tensor_copy(
+            out=bias_rows[:].rearrange("p (half c e) -> p half c e", half=HALVES, e=2),
+            in_=bias_bank[:].rearrange("p (half e c) -> p half c e", half=HALVES, e=2),
         )
 
-        pack_weight(nc, pools, ident, "a2", w_sb["a2"], codes["a2"], scales["a2"])
-        acc_a = second_layer(nc, pools, codes["ua"], scales["ua"], codes["a2"], scales["a2"])
-        a_sb = sbuf.tile([P, OUT], F32)
-        nc.vector.tensor_tensor(
-            out=a_sb[:].rearrange("p (c r) -> p c r", r=BLOCKS),
-            in0=acc_a[:].rearrange("p (r c) -> p c r", r=BLOCKS),
-            in1=bias_rows[:].rearrange("p (c r) -> p c r", r=BLOCKS),
-            op=ALU.add,
-        )
-        pack_weight(nc, pools, ident, "g2", w_sb["g2"], codes["g2"], scales["g2"])
-        acc_g = second_layer(nc, pools, codes["ug"], scales["ug"], codes["g2"], scales["g2"])
+        transpose_half("a1", 1, nc.vector.tensor_copy)
+        quantise_half("a1", 0)
+        transpose_half("g1", 0, nc.scalar.copy)
+        quantise_half("a1", 1)
+        transpose_half("g1", 1, nc.scalar.copy)
+        quantise_half("g1", 0)
+        transpose_half("a2", 0, nc.scalar.copy)
+        quantise_half("g1", 1)
+        first_layer("a")
+        transpose_half("a2", 1, nc.vector.tensor_copy)
+        quantise_half("a2", 0)
+        first_layer("g")
+        transpose_half("g2", 0, nc.scalar.copy)
+        group_hidden("a", 1.0)
+        quantise_half("a2", 1)
+        quantise("ua", 0, P)
+        transpose_half("g2", 1, nc.scalar.copy)
+        group_hidden("g", -1.0)
+        quantise_half("g2", 0)
+        quantise("ug", 0, P)
+        quantise_half("g2", 1)
+
+        for half in range(HALVES):
+            acc[half] = acc_pool.tile([P, PAIR], F32, tag="acc", name="acc_%d" % half)
+            second_layer("a", half, True, False)
         diff = sbuf.tile([P, OUT], F32)
-        nc.vector.tensor_tensor(
-            out=diff[:].rearrange("p (c r) -> p c r", r=BLOCKS),
-            in0=a_sb[:].rearrange("p (c r) -> p c r", r=BLOCKS),
-            in1=acc_g[:].rearrange("p (r c) -> p c r", r=BLOCKS),
-            op=ALU.subtract,
-        )
+        for half in range(HALVES):
+            second_layer("g", half, False, True)
+            cols = slice(half * PAIR, (half + 1) * PAIR)
+            nc.vector.tensor_tensor(
+                out=diff[:, cols].rearrange("p (c e) -> p c e", e=2),
+                in0=acc[half][:].rearrange("p (e c) -> p c e", e=2),
+                in1=bias_rows[:, cols].rearrange("p (c e) -> p c e", e=2),
+                op=ALU.add,
+            )
         nc.sync.dma_start(out=out_0, in_=diff[:])
 
         squares = sbuf.tile([P, OUT], F32)
@@ -210,14 +208,14 @@ def tile_phiaslossengine_pa_s_kernel(
         nc.scalar.activation(
             out=squares[:], in_=diff[:], func=ACT.Square, scale=1.0 / math.sqrt(OUT), accum_out=tension[:]
         )
-        t_bank = pools["bank"].tile([P, BANK], F32, tag="bank")
+        t_bank = banks.tile([P, BANK], F32, tag="bank")
         nc.tensor.transpose(t_bank[:, 0:P], tension[:, 0:1].to_broadcast([P, P]), ident[:])
         neg_max = sbuf.tile([P, 1], F32)
         nc.vector.tensor_reduce(out=neg_max[:], in_=t_bank[:, 0:P], axis=AXIS.X, op=ALU.max, negate=True)
 
         e_col = sbuf.tile([P, 1], F32)
         nc.scalar.activation(out=e_col[:], in_=tension[:], func=ACT.Exp, bias=neg_max[:], scale=1.0)
-        comb_bank = pools["bank"].tile([P, BANK], F32, tag="bank")
+        comb_bank = banks.tile([P, BANK], F32, tag="bank")
         nc.tensor.matmul(out=comb_bank[:], lhsT=e_col[:, 0:1].to_broadcast([P, P]), rhs=diff[:], start=True, stop=True)
 
         t_rows = sbuf.tile([P, P], F32)
@@ -226,8 +224,6 @@ def tile_phiaslossengine_pa_s_kernel(
         e_rows = sbuf.tile([P, P], F32)
         e_sum = sbuf.tile([P, 1], F32)
         nc.scalar.activation(out=e_rows[:], in_=t_rows[:], func=ACT.Exp, bias=neg_max[:], scale=1.0, accum_out=e_sum[:])
-        inv_sum = sbuf.tile([P, 1], F32)
-        nc.vector.reciprocal(out=inv_sum[:], in_=e_sum[:])
 
         t_sum = sbuf.tile([P, 1], F32)
         nc.vector.tensor_reduce(out=t_sum[:], in_=t_rows[:], axis=AXIS.X, op=ALU.add)
@@ -235,6 +231,8 @@ def tile_phiaslossengine_pa_s_kernel(
         nc.vector.tensor_scalar_mul(out=t_mean[:], in0=t_sum[:], scalar1=1.0 / P)
         nc.sync.dma_start(out=out_3.rearrange("(o n) -> o n", o=1), in_=t_mean[0:1, :])
 
+        inv_sum = sbuf.tile([P, 1], F32)
+        nc.vector.reciprocal(out=inv_sum[:], in_=e_sum[:])
         combined = sbuf.tile([P, OUT], F32)
         nc.vector.tensor_scalar_mul(out=combined[:], in0=comb_bank[:], scalar1=inv_sum[:, 0:1])
         nc.sync.dma_start(out=out_2, in_=combined[0:1, :])

@@ -21,6 +21,11 @@ HALVES = 2
 PAIR = 2 * P
 BANK = 512
 
+IDLE_COLUMNS = 256
+HEAD_PASSES = 8
+RUN_PASSES = 2
+TAIL_PASSES = 10
+
 FLOPS = 4 * 2 * P * K * 512 + 2 * P * OUT
 
 
@@ -32,9 +37,11 @@ def tile_phiaslossengine_pa_s_kernel(
     with ExitStack() as ctx:
         ctx.enter_context(tc.manual_schedule())
         sbuf = ctx.enter_context(tc.tile_pool(name="sbuf", bufs=1))
-        banks = ctx.enter_context(tc.psum_pool(name="banks", bufs=4))
+        banks = ctx.enter_context(tc.psum_pool(name="banks", bufs=3))
         z_pool = ctx.enter_context(tc.psum_pool(name="z", bufs=2))
         acc_pool = ctx.enter_context(tc.psum_pool(name="acc", bufs=2))
+
+        idle_pool = ctx.enter_context(tc.psum_pool(name="idle", bufs=1))
 
         h_sb = sbuf.tile([P, K], BF16)
         nc.sync.dma_start(out=h_sb[:], in_=hiddens)
@@ -54,6 +61,27 @@ def tile_phiaslossengine_pa_s_kernel(
                     out=small[label][:].rearrange("p (half e) -> p half e", half=HALVES),
                     in_=vector.rearrange("(half p e) -> p half e", half=HALVES, e=2),
                 )
+
+        zeros = sbuf.tile([P, IDLE_COLUMNS * PACK], BF16, align_bytes=64)
+        idle_codes = sbuf.tile([P, IDLE_COLUMNS], U32, align_bytes=64)
+        idle_scales = sbuf.tile([P, IDLE_COLUMNS], U8, align_bytes=64)
+        nc.vector.memset(zeros[:], 0.0)
+        nc.vector.quantize_mx(out=idle_codes[:].bitcast(FP8X4), scales=idle_scales[:], in_=zeros[:])
+        idle_bank = idle_pool.tile([P, IDLE_COLUMNS], F32)
+
+        def idle(passes):
+            for repeat in range(passes):
+                nc.tensor.matmul_mx(
+                    out=idle_bank[:],
+                    lhsT=idle_codes[:, 0:P].bitcast(FP8X4),
+                    lhsT_scale=idle_scales[:, 0:P],
+                    rhs=idle_codes[:].bitcast(FP8X4),
+                    rhs_scale=idle_scales[:],
+                    start=True,
+                    stop=True,
+                )
+
+        idle(HEAD_PASSES)
 
         ident = sbuf.tile([P, P], F32)
         make_identity(nc, ident[:])
@@ -167,17 +195,21 @@ def tile_phiaslossengine_pa_s_kernel(
         )
 
         transpose_half("a1", 1, nc.vector.tensor_copy)
+        idle(RUN_PASSES)
         quantise_half("a1", 0)
         transpose_half("g1", 0, nc.scalar.copy)
         quantise_half("a1", 1)
         transpose_half("g1", 1, nc.scalar.copy)
+        idle(RUN_PASSES)
         quantise_half("g1", 0)
         transpose_half("a2", 0, nc.scalar.copy)
         quantise_half("g1", 1)
         first_layer("a")
+        idle(RUN_PASSES)
         transpose_half("a2", 1, nc.vector.tensor_copy)
         quantise_half("a2", 0)
         first_layer("g")
+        idle(RUN_PASSES)
         transpose_half("g2", 0, nc.scalar.copy)
         group_hidden("a", 1.0)
         quantise_half("a2", 1)
@@ -191,6 +223,7 @@ def tile_phiaslossengine_pa_s_kernel(
         for half in range(HALVES):
             acc[half] = acc_pool.tile([P, PAIR], F32, tag="acc", name="acc_%d" % half)
             second_layer("a", half, True, False)
+        idle(RUN_PASSES)
         diff = sbuf.tile([P, OUT], F32)
         for half in range(HALVES):
             second_layer("g", half, False, True)
@@ -201,6 +234,7 @@ def tile_phiaslossengine_pa_s_kernel(
                 in1=bias_rows[:, cols].rearrange("p (c e) -> p c e", e=2),
                 op=ALU.add,
             )
+        idle(TAIL_PASSES)
         nc.sync.dma_start(out=out_0, in_=diff[:])
 
         squares = sbuf.tile([P, OUT], F32)

@@ -20,11 +20,12 @@ OUT = 512
 HALVES = 2
 PAIR = 2 * P
 BANK = 512
+I32 = mybir.dt.int32
 
 IDLE_COLUMNS = 256
-HEAD_PASSES = 8
+HEAD_PASSES = 6
 RUN_PASSES = 2
-TAIL_PASSES = 10
+TAIL_PASSES = 8
 
 FLOPS = 4 * 2 * P * K * 512 + 2 * P * OUT
 
@@ -65,7 +66,7 @@ def tile_phiaslossengine_pa_s_kernel(
         zeros = sbuf.tile([P, IDLE_COLUMNS * PACK], BF16, align_bytes=64)
         idle_codes = sbuf.tile([P, IDLE_COLUMNS], U32, align_bytes=64)
         idle_scales = sbuf.tile([P, IDLE_COLUMNS], U8, align_bytes=64)
-        nc.vector.memset(zeros[:], 0.0)
+        nc.vector.memset(zeros[:].bitcast(I32), 0)
         nc.vector.quantize_mx(out=idle_codes[:].bitcast(FP8X4), scales=idle_scales[:], in_=zeros[:])
         idle_bank = idle_pool.tile([P, IDLE_COLUMNS], F32)
 
@@ -249,8 +250,16 @@ def tile_phiaslossengine_pa_s_kernel(
 
         e_col = sbuf.tile([P, 1], F32)
         nc.scalar.activation(out=e_col[:], in_=tension[:], func=ACT.Exp, bias=neg_max[:], scale=1.0)
-        comb_bank = banks.tile([P, BANK], F32, tag="bank")
-        nc.tensor.matmul(out=comb_bank[:], lhsT=e_col[:, 0:1].to_broadcast([P, P]), rhs=diff[:], start=True, stop=True)
+        comb_bank = {}
+        for half in range(HALVES):
+            comb_bank[half] = banks.tile([P, BANK], F32, tag="bank", name="comb_bank_%d" % half)
+            nc.tensor.matmul(
+                out=comb_bank[half][:, 0:PAIR],
+                lhsT=e_col[:, 0:1].to_broadcast([P, P]),
+                rhs=diff[:, half * PAIR : (half + 1) * PAIR],
+                start=True,
+                stop=True,
+            )
 
         t_rows = sbuf.tile([P, P], F32)
         nc.vector.tensor_copy(out=t_rows[:], in_=t_bank[:, 0:P])
@@ -268,5 +277,6 @@ def tile_phiaslossengine_pa_s_kernel(
         inv_sum = sbuf.tile([P, 1], F32)
         nc.vector.reciprocal(out=inv_sum[:], in_=e_sum[:])
         combined = sbuf.tile([P, OUT], F32)
-        nc.vector.tensor_scalar_mul(out=combined[:], in0=comb_bank[:], scalar1=inv_sum[:, 0:1])
+        nc.vector.tensor_scalar_mul(out=combined[:, 0:PAIR], in0=comb_bank[0][:, 0:PAIR], scalar1=inv_sum[:, 0:1])
+        nc.scalar.activation(out=combined[:, PAIR:OUT], in_=comb_bank[1][:, 0:PAIR], func=ACT.Copy, scale=inv_sum[:, 0:1])
         nc.sync.dma_start(out=out_2, in_=combined[0:1, :])

@@ -23,8 +23,8 @@ BANK = 512
 I32 = mybir.dt.int32
 
 IDLE_COLUMNS = 256
-HEAD_PASSES = 6
-RUN_PASSES = 2
+HEAD_PASSES = 3
+LATE_PASSES = 4
 TAIL_PASSES = 8
 
 FLOPS = 4 * 2 * P * K * 512 + 2 * P * OUT
@@ -38,12 +38,12 @@ def tile_phiaslossengine_pa_s_kernel(
     with ExitStack() as ctx:
         ctx.enter_context(tc.manual_schedule())
         sbuf = ctx.enter_context(tc.tile_pool(name="sbuf", bufs=1))
-        banks = ctx.enter_context(tc.psum_pool(name="banks", bufs=3))
-        z_pool = ctx.enter_context(tc.psum_pool(name="z", bufs=2))
-        acc_pool = ctx.enter_context(tc.psum_pool(name="acc", bufs=2))
-
+        banks = ctx.enter_context(tc.psum_pool(name="banks", bufs=5))
+        mx_pool = ctx.enter_context(tc.psum_pool(name="mx", bufs=2))
         idle_pool = ctx.enter_context(tc.psum_pool(name="idle", bufs=1))
 
+        vec_rows = sbuf.tile([P, P], F32)
+        nc.vector.memset(vec_rows[:].bitcast(I32), 0)
         h_sb = sbuf.tile([P, K], BF16)
         nc.sync.dma_start(out=h_sb[:], in_=hiddens)
         w_sb = {}
@@ -54,15 +54,12 @@ def tile_phiaslossengine_pa_s_kernel(
                     out=w_sb[label][:, half * 2 * K : (half + 1) * 2 * K],
                     in_=weights[label][half * PAIR : (half + 1) * PAIR, :].rearrange("(p e) k -> p (e k)", e=2),
                 )
-        small = {}
-        with nc.allow_non_contiguous_dma(reason="512 values spread over 128 partitions"):
-            for label, vector in (("ba", ba2), ("bg", bg2), ("da", drive_a), ("dg", drive_g)):
-                small[label] = sbuf.tile([P, PACK], BF16, name="small_%s" % label)
-                nc.scalar.dma_start(
-                    out=small[label][:].rearrange("p (half e) -> p half e", half=HALVES),
-                    in_=vector.rearrange("(half p e) -> p half e", half=HALVES, e=2),
-                )
-
+            if label == "a1":
+                for i, vector in enumerate((ba2, bg2, drive_a, drive_g)):
+                    nc.sync.dma_start(
+                        out=vec_rows[HALVES * i : HALVES * (i + 1), :].bitcast(BF16),
+                        in_=vector.rearrange("(half w) -> half w", half=HALVES),
+                    )
         zeros = sbuf.tile([P, IDLE_COLUMNS * PACK], BF16, align_bytes=64)
         idle_codes = sbuf.tile([P, IDLE_COLUMNS], U32, align_bytes=64)
         idle_scales = sbuf.tile([P, IDLE_COLUMNS], U8, align_bytes=64)
@@ -89,10 +86,10 @@ def tile_phiaslossengine_pa_s_kernel(
         warm = sbuf.tile([P, 1], F32)
         nc.vector.memset(warm[:], 0.0)
         nc.scalar.activation(out=warm[:], in_=warm[:], func=ACT.Exp)
-        drive = {}
-        for net, label in (("a", "da"), ("g", "dg")):
-            drive[net] = sbuf.tile([P, PACK], F32, name="drive_%s" % net)
-            nc.gpsimd.tensor_copy(out=drive[net][:], in_=small[label][:])
+        vec_words = sbuf.tile([P, 4 * HALVES], F32)
+        small = {}
+        for i, label in enumerate(("ba", "bg", "a", "g")):
+            small[label] = vec_words[:].bitcast(BF16)[:, PACK * i : PACK * (i + 1)]
 
         grouped = {}
         codes = {}
@@ -135,7 +132,7 @@ def tile_phiaslossengine_pa_s_kernel(
 
         def first_layer(net):
             w1 = net + "1"
-            z = z_pool.tile([P, PACK * P], F32, tag="z")
+            z = mx_pool.tile([P, PACK * P], F32, tag="mx")
             for t in range(PACK):
                 cols = slice(t * P, (t + 1) * P)
                 nc.tensor.matmul_mx(
@@ -151,7 +148,7 @@ def tile_phiaslossengine_pa_s_kernel(
             for t in range(PACK):
                 cols = slice(t * P, (t + 1) * P)
                 nc.scalar.activation(
-                    out=planes[net][:, cols], in_=z[:, cols], func=ACT.Relu, bias=drive[net][:, t : t + 1], scale=1.0
+                    out=planes[net][:, cols], in_=z[:, cols], func=ACT.Relu, bias=small[net][:, t : t + 1], scale=1.0
                 )
 
         def group_hidden(net, sign):
@@ -182,49 +179,48 @@ def tile_phiaslossengine_pa_s_kernel(
             in_=h_bank[:, 0:PAIR].rearrange("p (khalf c) -> p c khalf", khalf=HALVES),
         )
         transpose_half("a1", 0, nc.scalar.copy)
+        quantise("h", 0, P)
+        transpose_half("a1", 1, nc.vector.tensor_copy)
 
+        vec_bank = banks.tile([P, BANK], F32, tag="bank")
+        nc.tensor.transpose(vec_bank[:, 0:P], vec_rows[:], ident[:])
+        nc.scalar.copy(out=vec_words[:], in_=vec_bank[:, 0 : 4 * HALVES])
+        quantise_half("a1", 0)
         bias_col = sbuf.tile([P, PACK], F32)
-        nc.vector.tensor_tensor(out=bias_col[:], in0=small["ba"][:], in1=small["bg"][:], op=ALU.subtract)
+        nc.gpsimd.tensor_tensor(out=bias_col[:], in0=small["ba"], in1=small["bg"], op=ALU.subtract)
+
+        transpose_half("g1", 0, nc.scalar.copy)
+        quantise_half("a1", 1)
+        transpose_half("g1", 1, nc.scalar.copy)
+        quantise_half("g1", 0)
         bias_bank = banks.tile([P, BANK], F32, tag="bank")
         for t in range(PACK):
             nc.tensor.transpose(bias_bank[:, t * P : (t + 1) * P], bias_col[:, t : t + 1].to_broadcast([P, P]), ident[:])
-        quantise("h", 0, P)
+        transpose_half("a2", 0, nc.scalar.copy)
+        first_layer("a")
+        quantise_half("g1", 1)
+        transpose_half("a2", 1, nc.vector.tensor_copy)
+        quantise_half("a2", 0)
+        first_layer("g")
+        group_hidden("a", 1.0)
+        transpose_half("g2", 0, nc.scalar.copy)
+        quantise_half("a2", 1)
+        transpose_half("g2", 1, nc.scalar.copy)
+        quantise("ua", 0, P)
+        group_hidden("g", -1.0)
         bias_rows = sbuf.tile([P, OUT], F32)
         nc.vector.tensor_copy(
             out=bias_rows[:].rearrange("p (half c e) -> p half c e", half=HALVES, e=2),
             in_=bias_bank[:].rearrange("p (half e c) -> p half c e", half=HALVES, e=2),
         )
-
-        transpose_half("a1", 1, nc.vector.tensor_copy)
-        idle(RUN_PASSES)
-        quantise_half("a1", 0)
-        transpose_half("g1", 0, nc.scalar.copy)
-        quantise_half("a1", 1)
-        transpose_half("g1", 1, nc.scalar.copy)
-        idle(RUN_PASSES)
-        quantise_half("g1", 0)
-        transpose_half("a2", 0, nc.scalar.copy)
-        quantise_half("g1", 1)
-        first_layer("a")
-        idle(RUN_PASSES)
-        transpose_half("a2", 1, nc.vector.tensor_copy)
-        quantise_half("a2", 0)
-        first_layer("g")
-        idle(RUN_PASSES)
-        transpose_half("g2", 0, nc.scalar.copy)
-        group_hidden("a", 1.0)
-        quantise_half("a2", 1)
-        quantise("ua", 0, P)
-        transpose_half("g2", 1, nc.scalar.copy)
-        group_hidden("g", -1.0)
         quantise_half("g2", 0)
         quantise("ug", 0, P)
         quantise_half("g2", 1)
+        idle(LATE_PASSES)
 
         for half in range(HALVES):
-            acc[half] = acc_pool.tile([P, PAIR], F32, tag="acc", name="acc_%d" % half)
+            acc[half] = mx_pool.tile([P, PAIR], F32, tag="mx", name="acc_%d" % half)
             second_layer("a", half, True, False)
-        idle(RUN_PASSES)
         diff = sbuf.tile([P, OUT], F32)
         for half in range(HALVES):
             second_layer("g", half, False, True)

@@ -24,8 +24,9 @@ I32 = mybir.dt.int32
 
 IDLE_COLUMNS = 256
 HEAD_PASSES = 3
-LATE_PASSES = 4
-TAIL_PASSES = 8
+LATE_PASSES = 6
+TAIL_PASSES = 6
+POST_PASSES = 4
 
 FLOPS = 4 * 2 * P * K * 512 + 2 * P * OUT
 
@@ -209,7 +210,7 @@ def tile_phiaslossengine_pa_s_kernel(
         quantise("ua", 0, P)
         group_hidden("g", -1.0)
         bias_rows = sbuf.tile([P, OUT], F32)
-        nc.vector.tensor_copy(
+        nc.scalar.copy(
             out=bias_rows[:].rearrange("p (half c e) -> p half c e", half=HALVES, e=2),
             in_=bias_bank[:].rearrange("p (half e c) -> p half c e", half=HALVES, e=2),
         )
@@ -235,12 +236,26 @@ def tile_phiaslossengine_pa_s_kernel(
         nc.sync.dma_start(out=out_0, in_=diff[:])
 
         squares = sbuf.tile([P, OUT], F32)
-        tension = sbuf.tile([P, 1], F32)
-        nc.scalar.activation(
-            out=squares[:], in_=diff[:], func=ACT.Square, scale=1.0 / math.sqrt(OUT), accum_out=tension[:]
-        )
+        part = {}
+        for half in range(HALVES):
+            cols = slice(half * PAIR, (half + 1) * PAIR)
+            part[half] = sbuf.tile([P, 1], F32, name="part_%d" % half)
+            nc.scalar.activation(
+                out=squares[:, cols], in_=diff[:, cols], func=ACT.Square, scale=1.0 / math.sqrt(OUT), accum_out=part[half][:]
+            )
         t_bank = banks.tile([P, BANK], F32, tag="bank")
-        nc.tensor.transpose(t_bank[:, 0:P], tension[:, 0:1].to_broadcast([P, P]), ident[:])
+        for half in range(HALVES):
+            nc.tensor.matmul(
+                out=t_bank[:, 0:P],
+                lhsT=part[half][:, 0:1].to_broadcast([P, P]),
+                rhs=ident[:],
+                is_transpose=True,
+                start=(half == 0),
+                stop=(half == HALVES - 1),
+            )
+        idle(POST_PASSES)
+        tension = sbuf.tile([P, 1], F32)
+        nc.scalar.activation(out=tension[:], in_=part[0][:], func=ACT.Identity, bias=part[1][:], scale=1.0)
         neg_max = sbuf.tile([P, 1], F32)
         nc.vector.tensor_reduce(out=neg_max[:], in_=t_bank[:, 0:P], axis=AXIS.X, op=ALU.max, negate=True)
 

@@ -22,11 +22,12 @@ PAIR = 2 * P
 BANK = 512
 I32 = mybir.dt.int32
 
-IDLE_COLUMNS = 256
-HEAD_PASSES = 3
-LATE_PASSES = 6
-TAIL_PASSES = 6
-POST_PASSES = 4
+IDLE_COLUMNS = 128
+HEAD_PASSES = 11
+RUN_PASSES = 2
+LATE_PASSES = 12
+TAIL_PASSES = 12
+POST_PASSES = 8
 
 FLOPS = 4 * 2 * P * K * 512 + 2 * P * OUT
 
@@ -43,6 +44,11 @@ def tile_phiaslossengine_pa_s_kernel(
         mx_pool = ctx.enter_context(tc.psum_pool(name="mx", bufs=2))
         idle_pool = ctx.enter_context(tc.psum_pool(name="idle", bufs=1))
 
+        zeros = sbuf.tile([P, IDLE_COLUMNS * PACK], BF16, align_bytes=64)
+        idle_codes = sbuf.tile([P, IDLE_COLUMNS], U32, align_bytes=64)
+        idle_scales = sbuf.tile([P, IDLE_COLUMNS], U8, align_bytes=64)
+        nc.vector.memset(zeros[:].bitcast(I32), 0)
+        nc.vector.quantize_mx(out=idle_codes[:].bitcast(FP8X4), scales=idle_scales[:], in_=zeros[:])
         vec_rows = sbuf.tile([P, P], F32)
         nc.vector.memset(vec_rows[:].bitcast(I32), 0)
         h_sb = sbuf.tile([P, K], BF16)
@@ -61,11 +67,6 @@ def tile_phiaslossengine_pa_s_kernel(
                         out=vec_rows[HALVES * i : HALVES * (i + 1), :].bitcast(BF16),
                         in_=vector.rearrange("(half w) -> half w", half=HALVES),
                     )
-        zeros = sbuf.tile([P, IDLE_COLUMNS * PACK], BF16, align_bytes=64)
-        idle_codes = sbuf.tile([P, IDLE_COLUMNS], U32, align_bytes=64)
-        idle_scales = sbuf.tile([P, IDLE_COLUMNS], U8, align_bytes=64)
-        nc.vector.memset(zeros[:].bitcast(I32), 0)
-        nc.vector.quantize_mx(out=idle_codes[:].bitcast(FP8X4), scales=idle_scales[:], in_=zeros[:])
         idle_bank = idle_pool.tile([P, IDLE_COLUMNS], F32)
 
         def idle(passes):
@@ -183,6 +184,7 @@ def tile_phiaslossengine_pa_s_kernel(
         quantise("h", 0, P)
         transpose_half("a1", 1, nc.vector.tensor_copy)
 
+        idle(RUN_PASSES)
         vec_bank = banks.tile([P, BANK], F32, tag="bank")
         nc.tensor.transpose(vec_bank[:, 0:P], vec_rows[:], ident[:])
         nc.scalar.copy(out=vec_words[:], in_=vec_bank[:, 0 : 4 * HALVES])
@@ -191,8 +193,10 @@ def tile_phiaslossengine_pa_s_kernel(
         nc.gpsimd.tensor_tensor(out=bias_col[:], in0=small["ba"], in1=small["bg"], op=ALU.subtract)
 
         transpose_half("g1", 0, nc.scalar.copy)
+        idle(RUN_PASSES)
         quantise_half("a1", 1)
         transpose_half("g1", 1, nc.scalar.copy)
+        idle(RUN_PASSES)
         quantise_half("g1", 0)
         bias_bank = banks.tile([P, BANK], F32, tag="bank")
         for t in range(PACK):
@@ -205,6 +209,7 @@ def tile_phiaslossengine_pa_s_kernel(
         first_layer("g")
         group_hidden("a", 1.0)
         transpose_half("g2", 0, nc.scalar.copy)
+        idle(RUN_PASSES)
         quantise_half("a2", 1)
         transpose_half("g2", 1, nc.scalar.copy)
         quantise("ua", 0, P)

@@ -23,11 +23,10 @@ BANK = 512
 I32 = mybir.dt.int32
 
 IDLE_COLUMNS = 128
-HEAD_PASSES = 11
-RUN_PASSES = 2
-LATE_PASSES = 12
-TAIL_PASSES = 12
-POST_PASSES = 8
+HEAD_PASSES = 10
+LATE_PASSES = 10
+TAIL_PASSES = 8
+POST_PASSES = 6
 
 FLOPS = 4 * 2 * P * K * 512 + 2 * P * OUT
 
@@ -184,7 +183,6 @@ def tile_phiaslossengine_pa_s_kernel(
         quantise("h", 0, P)
         transpose_half("a1", 1, nc.vector.tensor_copy)
 
-        idle(RUN_PASSES)
         vec_bank = banks.tile([P, BANK], F32, tag="bank")
         nc.tensor.transpose(vec_bank[:, 0:P], vec_rows[:], ident[:])
         nc.scalar.copy(out=vec_words[:], in_=vec_bank[:, 0 : 4 * HALVES])
@@ -193,10 +191,8 @@ def tile_phiaslossengine_pa_s_kernel(
         nc.gpsimd.tensor_tensor(out=bias_col[:], in0=small["ba"], in1=small["bg"], op=ALU.subtract)
 
         transpose_half("g1", 0, nc.scalar.copy)
-        idle(RUN_PASSES)
         quantise_half("a1", 1)
         transpose_half("g1", 1, nc.scalar.copy)
-        idle(RUN_PASSES)
         quantise_half("g1", 0)
         bias_bank = banks.tile([P, BANK], F32, tag="bank")
         for t in range(PACK):
@@ -209,7 +205,6 @@ def tile_phiaslossengine_pa_s_kernel(
         first_layer("g")
         group_hidden("a", 1.0)
         transpose_half("g2", 0, nc.scalar.copy)
-        idle(RUN_PASSES)
         quantise_half("a2", 1)
         transpose_half("g2", 1, nc.scalar.copy)
         quantise("ua", 0, P)

@@ -23,7 +23,8 @@ BANK = 512
 I32 = mybir.dt.int32
 
 IDLE_COLUMNS = 128
-HEAD_PASSES = 10
+HEAD_PASSES = 11
+RUN_PASSES = 1
 LATE_PASSES = 10
 TAIL_PASSES = 8
 POST_PASSES = 6
@@ -51,7 +52,6 @@ def tile_phiaslossengine_pa_s_kernel(
         vec_rows = sbuf.tile([P, P], F32)
         nc.vector.memset(vec_rows[:].bitcast(I32), 0)
         h_sb = sbuf.tile([P, K], BF16)
-        nc.sync.dma_start(out=h_sb[:], in_=hiddens)
         w_sb = {}
         for label in ("a1", "g1", "a2", "g2"):
             w_sb[label] = sbuf.tile([P, HALVES * 2 * K], BF16, name="w_%s" % label)
@@ -60,6 +60,8 @@ def tile_phiaslossengine_pa_s_kernel(
                     out=w_sb[label][:, half * 2 * K : (half + 1) * 2 * K],
                     in_=weights[label][half * PAIR : (half + 1) * PAIR, :].rearrange("(p e) k -> p (e k)", e=2),
                 )
+                if label == "a1" and half == 0:
+                    nc.sync.dma_start(out=h_sb[:], in_=hiddens)
             if label == "a1":
                 for i, vector in enumerate((ba2, bg2, drive_a, drive_g)):
                     nc.sync.dma_start(
@@ -119,6 +121,18 @@ def tile_phiaslossengine_pa_s_kernel(
                 in_=bank[:].rearrange("p (e khalf r) -> p e r khalf", e=2, khalf=HALVES),
             )
 
+        def transpose_split(label, half, engine_copies):
+            for e, engine_copy in enumerate(engine_copies):
+                block = 2 * half + e
+                bank = banks.tile([P, BANK], F32, tag="bank")
+                transpose_words(bank, 0, w_sb[label][:, block * K : (block + 1) * K])
+                engine_copy(
+                    out=grouped[label][:, block * P * PACK : (block + 1) * P * PACK]
+                    .bitcast(F32)
+                    .rearrange("p (r khalf) -> p r khalf", khalf=HALVES),
+                    in_=bank[:, 0:PAIR].rearrange("p (khalf r) -> p r khalf", khalf=HALVES),
+                )
+
         def quantise(label, first, columns):
             nc.vector.quantize_mx(
                 out=codes[label][:, first : first + columns].bitcast(FP8X4),
@@ -130,6 +144,7 @@ def tile_phiaslossengine_pa_s_kernel(
             quantise(label, half * PAIR, PAIR)
 
         planes = {}
+        hidden = {}
 
         def first_layer(net):
             w1 = net + "1"
@@ -145,18 +160,20 @@ def tile_phiaslossengine_pa_s_kernel(
                     start=True,
                     stop=True,
                 )
-            planes[net] = sbuf.tile([P, PACK * P], BF16, name="planes_%s" % net)
-            for t in range(PACK):
-                cols = slice(t * P, (t + 1) * P)
-                nc.scalar.activation(
-                    out=planes[net][:, cols], in_=z[:, cols], func=ACT.Relu, bias=small[net][:, t : t + 1], scale=1.0
-                )
+            hidden[net] = z
 
-        def group_hidden(net, sign):
-            nc.vector.tensor_scalar_mul(
-                out=grouped["u" + net][:].rearrange("p (c t) -> p c t", t=PACK),
-                in0=planes[net][:].rearrange("p (t c) -> p c t", t=PACK),
-                scalar1=sign,
+        def add_drive(net):
+            planes[net] = sbuf.tile([P, PACK * P], BF16, name="planes_%s" % net)
+            nc.vector.tensor_tensor(
+                out=planes[net][:].rearrange("p (c t) -> p c t", t=PACK),
+                in0=hidden[net][:].rearrange("p (t c) -> p c t", t=PACK),
+                in1=small[net].unsqueeze(1).to_broadcast([P, P, PACK]),
+                op=ALU.add,
+            )
+
+        def relu(net, sign):
+            nc.vector.tensor_scalar(
+                out=grouped["u" + net][:], in0=planes[net][:], scalar1=0.0, scalar2=sign, op0=ALU.max, op1=ALU.mult
             )
 
         acc = {}
@@ -173,49 +190,53 @@ def tile_phiaslossengine_pa_s_kernel(
                 stop=stop,
             )
 
+        transpose_split("a1", 0, (nc.scalar.copy, nc.vector.tensor_copy))
         h_bank = banks.tile([P, BANK], F32, tag="bank")
         transpose_words(h_bank, 0, h_sb[:])
         nc.vector.tensor_copy(
             out=grouped["h"][:].bitcast(F32).rearrange("p (c khalf) -> p c khalf", khalf=HALVES),
             in_=h_bank[:, 0:PAIR].rearrange("p (khalf c) -> p c khalf", khalf=HALVES),
         )
-        transpose_half("a1", 0, nc.scalar.copy)
+        idle(RUN_PASSES)
+        transpose_half("a1", 1, nc.scalar.copy)
+        quantise_half("a1", 0)
         quantise("h", 0, P)
-        transpose_half("a1", 1, nc.vector.tensor_copy)
 
         vec_bank = banks.tile([P, BANK], F32, tag="bank")
         nc.tensor.transpose(vec_bank[:, 0:P], vec_rows[:], ident[:])
         nc.scalar.copy(out=vec_words[:], in_=vec_bank[:, 0 : 4 * HALVES])
-        quantise_half("a1", 0)
         bias_col = sbuf.tile([P, PACK], F32)
         nc.gpsimd.tensor_tensor(out=bias_col[:], in0=small["ba"], in1=small["bg"], op=ALU.subtract)
-
-        transpose_half("g1", 0, nc.scalar.copy)
+        idle(RUN_PASSES)
         quantise_half("a1", 1)
+        transpose_half("g1", 0, nc.scalar.copy)
+        idle(RUN_PASSES)
         transpose_half("g1", 1, nc.scalar.copy)
         quantise_half("g1", 0)
+        first_layer("a")
+        transpose_half("a2", 0, nc.scalar.copy)
+        add_drive("a")
+        quantise_half("g1", 1)
+        relu("a", 1.0)
+        transpose_half("a2", 1, nc.scalar.copy)
+        quantise_half("a2", 0)
+        first_layer("g")
+        quantise("ua", 0, P)
+        transpose_half("g2", 0, nc.scalar.copy)
+        add_drive("g")
+        quantise_half("a2", 1)
+        relu("g", -1.0)
+        transpose_split("g2", 1, (nc.scalar.copy, nc.vector.tensor_copy))
         bias_bank = banks.tile([P, BANK], F32, tag="bank")
         for t in range(PACK):
             nc.tensor.transpose(bias_bank[:, t * P : (t + 1) * P], bias_col[:, t : t + 1].to_broadcast([P, P]), ident[:])
-        transpose_half("a2", 0, nc.scalar.copy)
-        first_layer("a")
-        quantise_half("g1", 1)
-        transpose_half("a2", 1, nc.vector.tensor_copy)
-        quantise_half("a2", 0)
-        first_layer("g")
-        group_hidden("a", 1.0)
-        transpose_half("g2", 0, nc.scalar.copy)
-        quantise_half("a2", 1)
-        transpose_half("g2", 1, nc.scalar.copy)
-        quantise("ua", 0, P)
-        group_hidden("g", -1.0)
         bias_rows = sbuf.tile([P, OUT], F32)
         nc.scalar.copy(
             out=bias_rows[:].rearrange("p (half c e) -> p half c e", half=HALVES, e=2),
             in_=bias_bank[:].rearrange("p (half e c) -> p half c e", half=HALVES, e=2),
         )
-        quantise_half("g2", 0)
         quantise("ug", 0, P)
+        quantise_half("g2", 0)
         quantise_half("g2", 1)
         idle(LATE_PASSES)
 

@@ -22,12 +22,12 @@ PAIR = 2 * P
 BANK = 512
 I32 = mybir.dt.int32
 
-IDLE_COLUMNS = 128
-HEAD_PASSES = 11
-RUN_PASSES = 1
-LATE_PASSES = 10
-TAIL_PASSES = 8
-POST_PASSES = 6
+IDLE_COLUMNS = 256
+FIRST_PASSES = 2
+HEAD_PASSES = 3
+LATE_PASSES = 6
+TAIL_PASSES = 6
+POST_PASSES = 5
 
 FLOPS = 4 * 2 * P * K * 512 + 2 * P * OUT
 
@@ -44,30 +44,48 @@ def tile_phiaslossengine_pa_s_kernel(
         mx_pool = ctx.enter_context(tc.psum_pool(name="mx", bufs=2))
         idle_pool = ctx.enter_context(tc.psum_pool(name="idle", bufs=1))
 
+        plain_zeros = sbuf.tile([P, P], F32)
+        nc.gpsimd.memset(plain_zeros[:], 0.0)
+        vec_rows = {}
+        for pair in ("drive", "bias"):
+            vec_rows[pair] = sbuf.tile([P, P], F32, name="rows_%s" % pair)
+            nc.vector.memset(vec_rows[pair][:].bitcast(I32), 0)
         zeros = sbuf.tile([P, IDLE_COLUMNS * PACK], BF16, align_bytes=64)
         idle_codes = sbuf.tile([P, IDLE_COLUMNS], U32, align_bytes=64)
         idle_scales = sbuf.tile([P, IDLE_COLUMNS], U8, align_bytes=64)
         nc.vector.memset(zeros[:].bitcast(I32), 0)
         nc.vector.quantize_mx(out=idle_codes[:].bitcast(FP8X4), scales=idle_scales[:], in_=zeros[:])
-        vec_rows = sbuf.tile([P, P], F32)
-        nc.vector.memset(vec_rows[:].bitcast(I32), 0)
-        h_sb = sbuf.tile([P, K], BF16)
+        def load_vectors(pair, vectors):
+            for i, vector in enumerate(vectors):
+                nc.sync.dma_start(
+                    out=vec_rows[pair][HALVES * i : HALVES * (i + 1), :].bitcast(BF16),
+                    in_=vector.rearrange("(half w) -> half w", half=HALVES),
+                )
+
         w_sb = {}
         for label in ("a1", "g1", "a2", "g2"):
             w_sb[label] = sbuf.tile([P, HALVES * 2 * K], BF16, name="w_%s" % label)
-            for half in range(HALVES):
-                nc.sync.dma_start(
-                    out=w_sb[label][:, half * 2 * K : (half + 1) * 2 * K],
-                    in_=weights[label][half * PAIR : (half + 1) * PAIR, :].rearrange("(p e) k -> p (e k)", e=2),
-                )
-                if label == "a1" and half == 0:
-                    nc.sync.dma_start(out=h_sb[:], in_=hiddens)
-            if label == "a1":
-                for i, vector in enumerate((ba2, bg2, drive_a, drive_g)):
-                    nc.sync.dma_start(
-                        out=vec_rows[HALVES * i : HALVES * (i + 1), :].bitcast(BF16),
-                        in_=vector.rearrange("(half w) -> half w", half=HALVES),
-                    )
+
+        def load_half(label, half):
+            nc.sync.dma_start(
+                out=w_sb[label][:, half * 2 * K : (half + 1) * 2 * K],
+                in_=weights[label][half * PAIR : (half + 1) * PAIR, :].rearrange("(p e) k -> p (e k)", e=2),
+            )
+
+        h_sb = sbuf.tile([P, K], BF16)
+        load_half("a1", 0)
+        nc.sync.dma_start(out=h_sb[:], in_=hiddens)
+        load_half("a1", 1)
+        load_half("g1", 0)
+        load_half("g1", 1)
+        load_vectors("drive", (drive_a, drive_g))
+        nc.sync.dma_start(
+            out=w_sb["a2"][:].rearrange("p (half ek) -> p half ek", half=HALVES),
+            in_=weights["a2"].rearrange("(half p e) k -> p half (e k)", half=HALVES, e=2),
+        )
+        load_vectors("bias", (ba2, bg2))
+        load_half("g2", 0)
+        load_half("g2", 1)
         idle_bank = idle_pool.tile([P, IDLE_COLUMNS], F32)
 
         def idle(passes):
@@ -82,6 +100,10 @@ def tile_phiaslossengine_pa_s_kernel(
                     stop=True,
                 )
 
+        for repeat in range(FIRST_PASSES):
+            nc.tensor.matmul(
+                out=idle_bank[:, 0:P], lhsT=plain_zeros[:], rhs=plain_zeros[:], start=True, stop=True
+            )
         idle(HEAD_PASSES)
 
         ident = sbuf.tile([P, P], F32)
@@ -89,10 +111,12 @@ def tile_phiaslossengine_pa_s_kernel(
         warm = sbuf.tile([P, 1], F32)
         nc.vector.memset(warm[:], 0.0)
         nc.scalar.activation(out=warm[:], in_=warm[:], func=ACT.Exp)
-        vec_words = sbuf.tile([P, 4 * HALVES], F32)
-        small = {}
-        for i, label in enumerate(("ba", "bg", "a", "g")):
-            small[label] = vec_words[:].bitcast(BF16)[:, PACK * i : PACK * (i + 1)]
+        def deal_vectors(pair):
+            bank = banks.tile([P, BANK], F32, tag="bank")
+            nc.tensor.transpose(bank[:, 0:P], vec_rows[pair][:], ident[:])
+            words = sbuf.tile([P, 2 * HALVES], F32, name="words_%s" % pair)
+            nc.scalar.copy(out=words[:], in_=bank[:, 0 : 2 * HALVES])
+            return [words[:].bitcast(BF16)[:, PACK * i : PACK * (i + 1)] for i in range(2)]
 
         grouped = {}
         codes = {}
@@ -197,21 +221,15 @@ def tile_phiaslossengine_pa_s_kernel(
             out=grouped["h"][:].bitcast(F32).rearrange("p (c khalf) -> p c khalf", khalf=HALVES),
             in_=h_bank[:, 0:PAIR].rearrange("p (khalf c) -> p c khalf", khalf=HALVES),
         )
-        idle(RUN_PASSES)
         transpose_half("a1", 1, nc.scalar.copy)
         quantise_half("a1", 0)
         quantise("h", 0, P)
 
-        vec_bank = banks.tile([P, BANK], F32, tag="bank")
-        nc.tensor.transpose(vec_bank[:, 0:P], vec_rows[:], ident[:])
-        nc.scalar.copy(out=vec_words[:], in_=vec_bank[:, 0 : 4 * HALVES])
-        bias_col = sbuf.tile([P, PACK], F32)
-        nc.gpsimd.tensor_tensor(out=bias_col[:], in0=small["ba"], in1=small["bg"], op=ALU.subtract)
-        idle(RUN_PASSES)
         quantise_half("a1", 1)
         transpose_half("g1", 0, nc.scalar.copy)
-        idle(RUN_PASSES)
         transpose_half("g1", 1, nc.scalar.copy)
+        small = {}
+        small["a"], small["g"] = deal_vectors("drive")
         quantise_half("g1", 0)
         first_layer("a")
         transpose_half("a2", 0, nc.scalar.copy)
@@ -219,6 +237,9 @@ def tile_phiaslossengine_pa_s_kernel(
         quantise_half("g1", 1)
         relu("a", 1.0)
         transpose_half("a2", 1, nc.scalar.copy)
+        bias_a, bias_g = deal_vectors("bias")
+        bias_col = sbuf.tile([P, PACK], F32)
+        nc.gpsimd.tensor_tensor(out=bias_col[:], in0=bias_a, in1=bias_g, op=ALU.subtract)
         quantise_half("a2", 0)
         first_layer("g")
         quantise("ua", 0, P)

@@ -24,8 +24,8 @@ I32 = mybir.dt.int32
 
 IDLE_COLUMNS = 256
 FIRST_PASSES = 2
-HEAD_PASSES = 3
-LATE_PASSES = 6
+HEAD_PASSES = 5
+LATE_PASSES = 5
 TAIL_PASSES = 6
 POST_PASSES = 5
 
@@ -77,13 +77,11 @@ def tile_phiaslossengine_pa_s_kernel(
         nc.sync.dma_start(out=h_sb[:], in_=hiddens)
         load_half("a1", 1)
         load_half("g1", 0)
-        load_half("g1", 1)
         load_vectors("drive", (drive_a, drive_g))
-        nc.sync.dma_start(
-            out=w_sb["a2"][:].rearrange("p (half ek) -> p half ek", half=HALVES),
-            in_=weights["a2"].rearrange("(half p e) k -> p half (e k)", half=HALVES, e=2),
-        )
+        load_half("g1", 1)
+        load_half("a2", 0)
         load_vectors("bias", (ba2, bg2))
+        load_half("a2", 1)
         load_half("g2", 0)
         load_half("g2", 1)
         idle_bank = idle_pool.tile([P, IDLE_COLUMNS], F32)
@@ -195,6 +193,21 @@ def tile_phiaslossengine_pa_s_kernel(
                 op=ALU.add,
             )
 
+        def relu_scalar(net):
+            planes[net] = sbuf.tile([P, PACK * P], BF16, name="planes_%s" % net)
+            for t in range(PACK):
+                cols = slice(t * P, (t + 1) * P)
+                nc.scalar.activation(
+                    out=planes[net][:, cols], in_=hidden[net][:, cols], func=ACT.Relu, bias=small[net][:, t : t + 1], scale=1.0
+                )
+
+        def group_hidden(net, sign):
+            nc.vector.tensor_scalar_mul(
+                out=grouped["u" + net][:].rearrange("p (c t) -> p c t", t=PACK),
+                in0=planes[net][:].rearrange("p (t c) -> p c t", t=PACK),
+                scalar1=sign,
+            )
+
         def relu(net, sign):
             nc.vector.tensor_scalar(
                 out=grouped["u" + net][:], in0=planes[net][:], scalar1=0.0, scalar2=sign, op0=ALU.max, op1=ALU.mult
@@ -224,40 +237,39 @@ def tile_phiaslossengine_pa_s_kernel(
         transpose_half("a1", 1, nc.scalar.copy)
         quantise_half("a1", 0)
         quantise("h", 0, P)
-
         quantise_half("a1", 1)
         transpose_half("g1", 0, nc.scalar.copy)
-        transpose_half("g1", 1, nc.scalar.copy)
         small = {}
         small["a"], small["g"] = deal_vectors("drive")
+        transpose_half("g1", 1, nc.scalar.copy)
         quantise_half("g1", 0)
         first_layer("a")
+        bias_a, bias_g = deal_vectors("bias")
+        bias_col = sbuf.tile([P, PACK], F32)
+        nc.gpsimd.tensor_tensor(out=bias_col[:], in0=bias_a, in1=bias_g, op=ALU.subtract)
         transpose_half("a2", 0, nc.scalar.copy)
         add_drive("a")
         quantise_half("g1", 1)
         relu("a", 1.0)
         transpose_half("a2", 1, nc.scalar.copy)
-        bias_a, bias_g = deal_vectors("bias")
-        bias_col = sbuf.tile([P, PACK], F32)
-        nc.gpsimd.tensor_tensor(out=bias_col[:], in0=bias_a, in1=bias_g, op=ALU.subtract)
-        quantise_half("a2", 0)
+        transpose_half("g2", 0, nc.scalar.copy)
         first_layer("g")
         quantise("ua", 0, P)
-        transpose_half("g2", 0, nc.scalar.copy)
-        add_drive("g")
-        quantise_half("a2", 1)
-        relu("g", -1.0)
-        transpose_split("g2", 1, (nc.scalar.copy, nc.vector.tensor_copy))
         bias_bank = banks.tile([P, BANK], F32, tag="bank")
         for t in range(PACK):
             nc.tensor.transpose(bias_bank[:, t * P : (t + 1) * P], bias_col[:, t : t + 1].to_broadcast([P, P]), ident[:])
+        quantise_half("a2", 0)
+        add_drive("g")
+        quantise_half("a2", 1)
+        relu("g", -1.0)
+        transpose_split("g2", 1, (nc.scalar.copy, nc.scalar.copy))
         bias_rows = sbuf.tile([P, OUT], F32)
         nc.scalar.copy(
             out=bias_rows[:].rearrange("p (half c e) -> p half c e", half=HALVES, e=2),
             in_=bias_bank[:].rearrange("p (half e c) -> p half c e", half=HALVES, e=2),
         )
-        quantise("ug", 0, P)
         quantise_half("g2", 0)
+        quantise("ug", 0, P)
         quantise_half("g2", 1)
         idle(LATE_PASSES)
 
@@ -280,11 +292,19 @@ def tile_phiaslossengine_pa_s_kernel(
         squares = sbuf.tile([P, OUT], F32)
         part = {}
         for half in range(HALVES):
-            cols = slice(half * PAIR, (half + 1) * PAIR)
             part[half] = sbuf.tile([P, 1], F32, name="part_%d" % half)
-            nc.scalar.activation(
-                out=squares[:, cols], in_=diff[:, cols], func=ACT.Square, scale=1.0 / math.sqrt(OUT), accum_out=part[half][:]
-            )
+        nc.scalar.activation(
+            out=squares[:, 0:PAIR], in_=diff[:, 0:PAIR], func=ACT.Square, scale=1.0 / math.sqrt(OUT), accum_out=part[0][:]
+        )
+        nc.vector.scalar_tensor_tensor(
+            out=squares[:, PAIR:OUT],
+            in0=diff[:, PAIR:OUT],
+            scalar=1.0 / OUT,
+            in1=diff[:, PAIR:OUT],
+            op0=ALU.mult,
+            op1=ALU.mult,
+            accum_out=part[1][:],
+        )
         t_bank = banks.tile([P, BANK], F32, tag="bank")
         for half in range(HALVES):
             nc.tensor.matmul(
@@ -303,13 +323,14 @@ def tile_phiaslossengine_pa_s_kernel(
 
         e_col = sbuf.tile([P, 1], F32)
         nc.scalar.activation(out=e_col[:], in_=tension[:], func=ACT.Exp, bias=neg_max[:], scale=1.0)
+        pieces = ((0, PAIR), (PAIR, PAIR + P), (PAIR + P, OUT))
         comb_bank = {}
-        for half in range(HALVES):
-            comb_bank[half] = banks.tile([P, BANK], F32, tag="bank", name="comb_bank_%d" % half)
+        for first, end in pieces:
+            comb_bank[first] = banks.tile([P, BANK], F32, tag="bank", name="comb_bank_%d" % first)
             nc.tensor.matmul(
-                out=comb_bank[half][:, 0:PAIR],
+                out=comb_bank[first][:, 0 : end - first],
                 lhsT=e_col[:, 0:1].to_broadcast([P, P]),
-                rhs=diff[:, half * PAIR : (half + 1) * PAIR],
+                rhs=diff[:, first:end],
                 start=True,
                 stop=True,
             )
@@ -330,6 +351,8 @@ def tile_phiaslossengine_pa_s_kernel(
         inv_sum = sbuf.tile([P, 1], F32)
         nc.vector.reciprocal(out=inv_sum[:], in_=e_sum[:])
         combined = sbuf.tile([P, OUT], F32)
-        nc.vector.tensor_scalar_mul(out=combined[:, 0:PAIR], in0=comb_bank[0][:, 0:PAIR], scalar1=inv_sum[:, 0:1])
-        nc.scalar.activation(out=combined[:, PAIR:OUT], in_=comb_bank[1][:, 0:PAIR], func=ACT.Copy, scale=inv_sum[:, 0:1])
+        for first, end in pieces:
+            nc.vector.tensor_scalar_mul(
+                out=combined[:, first:end], in0=comb_bank[first][:, 0 : end - first], scalar1=inv_sum[:, 0:1]
+            )
         nc.sync.dma_start(out=out_2, in_=combined[0:1, :])

@@ -76,8 +76,8 @@ def tile_phiaslossengine_pa_s_kernel(
         load_half("a1", 0)
         nc.sync.dma_start(out=h_sb[:], in_=hiddens)
         load_half("a1", 1)
-        load_half("g1", 0)
         load_vectors("drive", (drive_a, drive_g))
+        load_half("g1", 0)
         load_half("g1", 1)
         load_half("a2", 0)
         load_vectors("bias", (ba2, bg2))
@@ -227,49 +227,49 @@ def tile_phiaslossengine_pa_s_kernel(
                 stop=stop,
             )
 
-        transpose_split("a1", 0, (nc.scalar.copy, nc.vector.tensor_copy))
+        transpose_half("a1", 0, nc.scalar.copy)
         h_bank = banks.tile([P, BANK], F32, tag="bank")
         transpose_words(h_bank, 0, h_sb[:])
         nc.vector.tensor_copy(
             out=grouped["h"][:].bitcast(F32).rearrange("p (c khalf) -> p c khalf", khalf=HALVES),
             in_=h_bank[:, 0:PAIR].rearrange("p (khalf c) -> p c khalf", khalf=HALVES),
         )
-        transpose_half("a1", 1, nc.scalar.copy)
         quantise_half("a1", 0)
+        transpose_half("a1", 1, nc.scalar.copy)
+        small = {}
+        small["a"], small["g"] = deal_vectors("drive")
         quantise("h", 0, P)
         quantise_half("a1", 1)
         transpose_half("g1", 0, nc.scalar.copy)
-        small = {}
-        small["a"], small["g"] = deal_vectors("drive")
-        transpose_half("g1", 1, nc.scalar.copy)
-        quantise_half("g1", 0)
+        transpose_split("g1", 1, (nc.scalar.copy, nc.vector.tensor_copy))
         first_layer("a")
+        quantise_half("g1", 0)
+        relu_scalar("a")
         bias_a, bias_g = deal_vectors("bias")
         bias_col = sbuf.tile([P, PACK], F32)
         nc.gpsimd.tensor_tensor(out=bias_col[:], in0=bias_a, in1=bias_g, op=ALU.subtract)
         transpose_half("a2", 0, nc.scalar.copy)
-        add_drive("a")
         quantise_half("g1", 1)
-        relu("a", 1.0)
-        transpose_half("a2", 1, nc.scalar.copy)
-        transpose_half("g2", 0, nc.scalar.copy)
         first_layer("g")
+        transpose_half("a2", 1, nc.scalar.copy)
+        group_hidden("a", 1.0)
+        add_drive("g")
+        quantise_half("a2", 0)
         quantise("ua", 0, P)
+        transpose_half("g2", 0, nc.scalar.copy)
+        relu("g", -1.0)
+        quantise_half("a2", 1)
         bias_bank = banks.tile([P, BANK], F32, tag="bank")
         for t in range(PACK):
             nc.tensor.transpose(bias_bank[:, t * P : (t + 1) * P], bias_col[:, t : t + 1].to_broadcast([P, P]), ident[:])
-        quantise_half("a2", 0)
-        add_drive("g")
-        quantise_half("a2", 1)
-        relu("g", -1.0)
-        transpose_split("g2", 1, (nc.scalar.copy, nc.scalar.copy))
+        quantise_half("g2", 0)
+        quantise("ug", 0, P)
+        transpose_half("g2", 1, nc.scalar.copy)
         bias_rows = sbuf.tile([P, OUT], F32)
         nc.scalar.copy(
             out=bias_rows[:].rearrange("p (half c e) -> p half c e", half=HALVES, e=2),
             in_=bias_bank[:].rearrange("p (half e c) -> p half c e", half=HALVES, e=2),
         )
-        quantise_half("g2", 0)
-        quantise("ug", 0, P)
         quantise_half("g2", 1)
         idle(LATE_PASSES)
 

from contextlib import ExitStack
import math

import concourse.mybir as mybir
from concourse.masks import make_identity

F32 = mybir.dt.float32
BF16 = mybir.dt.bfloat16
U32 = mybir.dt.uint32
U8 = mybir.dt.uint8
FP8X4 = mybir.dt.float8_e4m3fn_x4
ACT = mybir.ActivationFunctionType
ALU = mybir.AluOpType
AXIS = mybir.AxisListType

P = 128
PACK = 4
K = P * PACK
OUT = 512
HALVES = 2
PAIR = 2 * P
BANK = 512
I32 = mybir.dt.int32

IDLE_COLUMNS = 256
FIRST_PASSES = 2
HEAD_PASSES = 5
LATE_PASSES = 5
TAIL_PASSES = 6
POST_PASSES = 5

FLOPS = 4 * 2 * P * K * 512 + 2 * P * OUT


def tile_phiaslossengine_pa_s_kernel(
    tc, hiddens, Wa1h, drive_a, Wa2, ba2, Wg1h, drive_g, Wg2, bg2, out_0, out_1, out_2, out_3
):
    nc = tc.nc
    weights = {"a1": Wa1h, "g1": Wg1h, "a2": Wa2, "g2": Wg2}
    with ExitStack() as ctx:
        ctx.enter_context(tc.manual_schedule())
        sbuf = ctx.enter_context(tc.tile_pool(name="sbuf", bufs=1))
        banks = ctx.enter_context(tc.psum_pool(name="banks", bufs=5))
        mx_pool = ctx.enter_context(tc.psum_pool(name="mx", bufs=2))
        idle_pool = ctx.enter_context(tc.psum_pool(name="idle", bufs=1))

        plain_zeros = sbuf.tile([P, P], F32)
        nc.gpsimd.memset(plain_zeros[:], 0.0)
        vec_rows = {}
        for pair in ("drive", "bias"):
            vec_rows[pair] = sbuf.tile([P, P], F32, name="rows_%s" % pair)
            nc.vector.memset(vec_rows[pair][:].bitcast(I32), 0)
        zeros = sbuf.tile([P, IDLE_COLUMNS * PACK], BF16, align_bytes=64)
        idle_codes = sbuf.tile([P, IDLE_COLUMNS], U32, align_bytes=64)
        idle_scales = sbuf.tile([P, IDLE_COLUMNS], U8, align_bytes=64)
        nc.vector.memset(zeros[:].bitcast(I32), 0)
        nc.vector.quantize_mx(out=idle_codes[:].bitcast(FP8X4), scales=idle_scales[:], in_=zeros[:])
        def load_vectors(pair, vectors):
            for i, vector in enumerate(vectors):
                nc.sync.dma_start(
                    out=vec_rows[pair][HALVES * i : HALVES * (i + 1), :].bitcast(BF16),
                    in_=vector.rearrange("(half w) -> half w", half=HALVES),
                )

        w_sb = {}
        for label in ("a1", "g1", "a2", "g2"):
            w_sb[label] = sbuf.tile([P, HALVES * 2 * K], BF16, name="w_%s" % label)

        def load_half(label, half):
            nc.sync.dma_start(
                out=w_sb[label][:, half * 2 * K : (half + 1) * 2 * K],
                in_=weights[label][half * PAIR : (half + 1) * PAIR, :].rearrange("(p e) k -> p (e k)", e=2),
            )

        h_sb = sbuf.tile([P, K], BF16)
        load_half("a1", 0)
        nc.sync.dma_start(out=h_sb[:], in_=hiddens)
        load_half("a1", 1)
        load_vectors("drive", (drive_a, drive_g))
        load_half("g1", 0)
        load_half("g1", 1)
        load_half("a2", 0)
        load_vectors("bias", (ba2, bg2))
        load_half("a2", 1)
        load_half("g2", 0)
        load_half("g2", 1)
        idle_bank = idle_pool.tile([P, IDLE_COLUMNS], F32)

        def idle(passes):
            for repeat in range(passes):
                nc.tensor.matmul_mx(
                    out=idle_bank[:],
                    lhsT=idle_codes[:, 0:P].bitcast(FP8X4),
                    lhsT_scale=idle_scales[:, 0:P],
                    rhs=idle_codes[:].bitcast(FP8X4),
                    rhs_scale=idle_scales[:],
                    start=True,
                    stop=True,
                )

        for repeat in range(FIRST_PASSES):
            nc.tensor.matmul(
                out=idle_bank[:, 0:P], lhsT=plain_zeros[:], rhs=plain_zeros[:], start=True, stop=True
            )
        idle(HEAD_PASSES)

        ident = sbuf.tile([P, P], F32)
        make_identity(nc, ident[:])
        warm = sbuf.tile([P, 1], F32)
        nc.vector.memset(warm[:], 0.0)
        nc.scalar.activation(out=warm[:], in_=warm[:], func=ACT.Exp)
        def deal_vectors(pair):
            bank = banks.tile([P, BANK], F32, tag="bank")
            nc.tensor.transpose(bank[:, 0:P], vec_rows[pair][:], ident[:])
            words = sbuf.tile([P, 2 * HALVES], F32, name="words_%s" % pair)
            nc.scalar.copy(out=words[:], in_=bank[:, 0 : 2 * HALVES])
            return [words[:].bitcast(BF16)[:, PACK * i : PACK * (i + 1)] for i in range(2)]

        grouped = {}
        codes = {}
        scales = {}
        for label, columns in (("h", P), ("ua", P), ("ug", P), ("a1", K), ("g1", K), ("a2", OUT), ("g2", OUT)):
            grouped[label] = sbuf.tile([P, columns * PACK], BF16, align_bytes=64, name="grouped_%s" % label)
            codes[label] = sbuf.tile([P, columns], U32, align_bytes=64, name="codes_%s" % label)
            scales[label] = sbuf.tile([P, columns], U8, align_bytes=64, name="scales_%s" % label)

        def transpose_words(bank, first, rows_bf16):
            words = rows_bf16.bitcast(F32)
            for khalf in range(HALVES):
                nc.tensor.transpose(
                    bank[:, first + khalf * P : first + (khalf + 1) * P], words[:, khalf * P : (khalf + 1) * P], ident[:]
                )

        def transpose_half(label, half, engine_copy):
            bank = banks.tile([P, BANK], F32, tag="bank")
            for e in range(2):
                block = 2 * half + e
                transpose_words(bank, e * PAIR, w_sb[label][:, block * K : (block + 1) * K])
            engine_copy(
                out=grouped[label][:, half * PAIR * PACK : (half + 1) * PAIR * PACK]
                .bitcast(F32)
                .rearrange("p (e r khalf) -> p e r khalf", e=2, khalf=HALVES),
                in_=bank[:].rearrange("p (e khalf r) -> p e r khalf", e=2, khalf=HALVES),
            )

        def transpose_split(label, half, engine_copies):
            for e, engine_copy in enumerate(engine_copies):
                block = 2 * half + e
                bank = banks.tile([P, BANK], F32, tag="bank")
                transpose_words(bank, 0, w_sb[label][:, block * K : (block + 1) * K])
                engine_copy(
                    out=grouped[label][:, block * P * PACK : (block + 1) * P * PACK]
                    .bitcast(F32)
                    .rearrange("p (r khalf) -> p r khalf", khalf=HALVES),
                    in_=bank[:, 0:PAIR].rearrange("p (khalf r) -> p r khalf", khalf=HALVES),
                )

        def quantise(label, first, columns):
            nc.vector.quantize_mx(
                out=codes[label][:, first : first + columns].bitcast(FP8X4),
                scales=scales[label][:, first : first + columns],
                in_=grouped[label][:, first * PACK : (first + columns) * PACK],
            )

        def quantise_half(label, half):
            quantise(label, half * PAIR, PAIR)

        planes = {}
        hidden = {}

        def first_layer(net):
            w1 = net + "1"
            z = mx_pool.tile([P, PACK * P], F32, tag="mx")
            for t in range(PACK):
                cols = slice(t * P, (t + 1) * P)
                nc.tensor.matmul_mx(
                    out=z[:, cols],
                    lhsT=codes[w1][:, cols].bitcast(FP8X4),
                    lhsT_scale=scales[w1][:, cols],
                    rhs=codes["h"][:].bitcast(FP8X4),
                    rhs_scale=scales["h"][:],
                    start=True,
                    stop=True,
                )
            hidden[net] = z

        def add_drive(net):
            planes[net] = sbuf.tile([P, PACK * P], BF16, name="planes_%s" % net)
            nc.vector.tensor_tensor(
                out=planes[net][:].rearrange("p (c t) -> p c t", t=PACK),
                in0=hidden[net][:].rearrange("p (t c) -> p c t", t=PACK),
                in1=small[net].unsqueeze(1).to_broadcast([P, P, PACK]),
                op=ALU.add,
            )

        def relu_scalar(net):
            planes[net] = sbuf.tile([P, PACK * P], BF16, name="planes_%s" % net)
            for t in range(PACK):
                cols = slice(t * P, (t + 1) * P)
                nc.scalar.activation(
                    out=planes[net][:, cols], in_=hidden[net][:, cols], func=ACT.Relu, bias=small[net][:, t : t + 1], scale=1.0
                )

        def group_hidden(net, sign):
            nc.vector.tensor_scalar_mul(
                out=grouped["u" + net][:].rearrange("p (c t) -> p c t", t=PACK),
                in0=planes[net][:].rearrange("p (t c) -> p c t", t=PACK),
                scalar1=sign,
            )

        def relu(net, sign):
            nc.vector.tensor_scalar(
                out=grouped["u" + net][:], in0=planes[net][:], scalar1=0.0, scalar2=sign, op0=ALU.max, op1=ALU.mult
            )

        acc = {}

        def second_layer(net, half, start, stop):
            cols = slice(half * PAIR, (half + 1) * PAIR)
            nc.tensor.matmul_mx(
                out=acc[half][:],
                lhsT=codes["u" + net][:].bitcast(FP8X4),
                lhsT_scale=scales["u" + net][:],
                rhs=codes[net + "2"][:, cols].bitcast(FP8X4),
                rhs_scale=scales[net + "2"][:, cols],
                start=start,
                stop=stop,
            )

        transpose_half("a1", 0, nc.scalar.copy)
        h_bank = banks.tile([P, BANK], F32, tag="bank")
        transpose_words(h_bank, 0, h_sb[:])
        nc.vector.tensor_copy(
            out=grouped["h"][:].bitcast(F32).rearrange("p (c khalf) -> p c khalf", khalf=HALVES),
            in_=h_bank[:, 0:PAIR].rearrange("p (khalf c) -> p c khalf", khalf=HALVES),
        )
        quantise_half("a1", 0)
        transpose_half("a1", 1, nc.scalar.copy)
        small = {}
        small["a"], small["g"] = deal_vectors("drive")
        quantise("h", 0, P)
        quantise_half("a1", 1)
        transpose_half("g1", 0, nc.scalar.copy)
        transpose_split("g1", 1, (nc.scalar.copy, nc.vector.tensor_copy))
        first_layer("a")
        quantise_half("g1", 0)
        relu_scalar("a")
        bias_a, bias_g = deal_vectors("bias")
        bias_col = sbuf.tile([P, PACK], F32)
        nc.gpsimd.tensor_tensor(out=bias_col[:], in0=bias_a, in1=bias_g, op=ALU.subtract)
        transpose_half("a2", 0, nc.scalar.copy)
        quantise_half("g1", 1)
        first_layer("g")
        transpose_half("a2", 1, nc.scalar.copy)
        group_hidden("a", 1.0)
        add_drive("g")
        quantise_half("a2", 0)
        quantise("ua", 0, P)
        transpose_half("g2", 0, nc.scalar.copy)
        relu("g", -1.0)
        quantise_half("a2", 1)
        bias_bank = banks.tile([P, BANK], F32, tag="bank")
        for t in range(PACK):
            nc.tensor.transpose(bias_bank[:, t * P : (t + 1) * P], bias_col[:, t : t + 1].to_broadcast([P, P]), ident[:])
        quantise_half("g2", 0)
        quantise("ug", 0, P)
        transpose_half("g2", 1, nc.scalar.copy)
        bias_rows = sbuf.tile([P, OUT], F32)
        nc.scalar.copy(
            out=bias_rows[:].rearrange("p (half c e) -> p half c e", half=HALVES, e=2),
            in_=bias_bank[:].rearrange("p (half e c) -> p half c e", half=HALVES, e=2),
        )
        quantise_half("g2", 1)
        idle(LATE_PASSES)

        for half in range(HALVES):
            acc[half] = mx_pool.tile([P, PAIR], F32, tag="mx", name="acc_%d" % half)
            second_layer("a", half, True, False)
        diff = sbuf.tile([P, OUT], F32)
        for half in range(HALVES):
            second_layer("g", half, False, True)
            cols = slice(half * PAIR, (half + 1) * PAIR)
            nc.vector.tensor_tensor(
                out=diff[:, cols].rearrange("p (c e) -> p c e", e=2),
                in0=acc[half][:].rearrange("p (e c) -> p c e", e=2),
                in1=bias_rows[:, cols].rearrange("p (c e) -> p c e", e=2),
                op=ALU.add,
            )
        idle(TAIL_PASSES)
        nc.sync.dma_start(out=out_0, in_=diff[:])

        squares = sbuf.tile([P, OUT], F32)
        part = {}
        for half in range(HALVES):
            part[half] = sbuf.tile([P, 1], F32, name="part_%d" % half)
        nc.scalar.activation(
            out=squares[:, 0:PAIR], in_=diff[:, 0:PAIR], func=ACT.Square, scale=1.0 / math.sqrt(OUT), accum_out=part[0][:]
        )
        nc.vector.scalar_tensor_tensor(
            out=squares[:, PAIR:OUT],
            in0=diff[:, PAIR:OUT],
            scalar=1.0 / OUT,
            in1=diff[:, PAIR:OUT],
            op0=ALU.mult,
            op1=ALU.mult,
            accum_out=part[1][:],
        )
        t_bank = banks.tile([P, BANK], F32, tag="bank")
        for half in range(HALVES):
            nc.tensor.matmul(
                out=t_bank[:, 0:P],
                lhsT=part[half][:, 0:1].to_broadcast([P, P]),
                rhs=ident[:],
                is_transpose=True,
                start=(half == 0),
                stop=(half == HALVES - 1),
            )
        idle(POST_PASSES)
        tension = sbuf.tile([P, 1], F32)
        nc.scalar.activation(out=tension[:], in_=part[0][:], func=ACT.Identity, bias=part[1][:], scale=1.0)
        neg_max = sbuf.tile([P, 1], F32)
        nc.vector.tensor_reduce(out=neg_max[:], in_=t_bank[:, 0:P], axis=AXIS.X, op=ALU.max, negate=True)

        e_col = sbuf.tile([P, 1], F32)
        nc.scalar.activation(out=e_col[:], in_=tension[:], func=ACT.Exp, bias=neg_max[:], scale=1.0)
        pieces = ((0, PAIR), (PAIR, PAIR + P), (PAIR + P, OUT))
        comb_bank = {}
        for first, end in pieces:
            comb_bank[first] = banks.tile([P, BANK], F32, tag="bank", name="comb_bank_%d" % first)
            nc.tensor.matmul(
                out=comb_bank[first][:, 0 : end - first],
                lhsT=e_col[:, 0:1].to_broadcast([P, P]),
                rhs=diff[:, first:end],
                start=True,
                stop=True,
            )

        t_rows = sbuf.tile([P, P], F32)
        nc.vector.tensor_copy(out=t_rows[:], in_=t_bank[:, 0:P])
        nc.sync.dma_start(out=out_1.rearrange("n o -> o n"), in_=t_rows[0:1, :])
        e_rows = sbuf.tile([P, P], F32)
        e_sum = sbuf.tile([P, 1], F32)
        nc.scalar.activation(out=e_rows[:], in_=t_rows[:], func=ACT.Exp, bias=neg_max[:], scale=1.0, accum_out=e_sum[:])

        t_sum = sbuf.tile([P, 1], F32)
        nc.vector.tensor_reduce(out=t_sum[:], in_=t_rows[:], axis=AXIS.X, op=ALU.add)
        t_mean = sbuf.tile([P, 1], F32)
        nc.vector.tensor_scalar_mul(out=t_mean[:], in0=t_sum[:], scalar1=1.0 / P)
        nc.sync.dma_start(out=out_3.rearrange("(o n) -> o n", o=1), in_=t_mean[0:1, :])

        inv_sum = sbuf.tile([P, 1], F32)
        nc.vector.reciprocal(out=inv_sum[:], in_=e_sum[:])
        combined = sbuf.tile([P, OUT], F32)
        for first, end in pieces:
            nc.vector.tensor_scalar_mul(
                out=combined[:, first:end], in0=comb_bank[first][:, 0 : end - first], scalar1=inv_sum[:, 0:1]
            )
        nc.sync.dma_start(out=out_2, in_=combined[0:1, :])
